import numpy as np
import ml_dtypes


def mxq(x, axis, fmt="e4m3"):
    dtype, down = {"e4m3": (ml_dtypes.float8_e4m3fn, 7), "e5m2": (ml_dtypes.float8_e5m2, 14)}[fmt]
    v = np.moveaxis(np.asarray(x, np.float32).astype(ml_dtypes.bfloat16).astype(np.float64), axis, -1)
    blocks = v.reshape(v.shape[:-1] + (-1, 32))
    amax = np.abs(blocks).max(-1, keepdims=True)
    byte = np.maximum(np.where(amax > 0, np.frexp(amax)[1] - 1 + 127, 0) - down, 1)
    scale = np.exp2(byte - 127.0)
    codes = (blocks / scale).astype(np.float32).astype(dtype).astype(np.float64)
    return np.moveaxis((codes * scale).reshape(v.shape), -1, axis)


WIDE = False


def mx_kscale(k):
    if not WIDE:
        return np.ones(k)
    levels = np.array([10, -10, 5, -5, 0])
    if k % 512:
        return np.exp2(np.random.permutation(np.resize(levels, k // 32))).repeat(32)
    a = np.empty((k // 512, 16))
    for p in range(k // 512):
        a[p, :8] = np.random.permutation(np.resize(levels, 8))
        for g in range(8):
            far = levels[np.abs(levels - a[p, g]) >= 10]
            a[p, g + 8] = far[np.random.randint(len(far))]
    return np.exp2(a.ravel()).repeat(32)


BF16 = ml_dtypes.bfloat16


def bf(x):
    return np.asarray(x, np.float32).astype(BF16)


def f64(x):
    return np.asarray(x).astype(np.float64)


B, D, S, N = 4096, 1024, 2, 128
DS = D // S
EPS = 1e-12


def setup_inputs():
    s, t = mx_kscale(D), mx_kscale(D)
    return {"h": bf(np.random.standard_normal((B, D)) * s),
            "x2f": bf(np.random.standard_normal((B, D)) * t),
            "vu": bf(np.random.standard_normal((N, S, DS)) * 2.0 / np.sqrt(DS) / t.reshape(S, DS)),
            "w_f": bf(np.random.standard_normal((D, D)) / np.sqrt(D) * t[:, None] / s),
            "b_f": bf(np.random.standard_normal(D) * 0.2 * t),
            "bh": bf(1.0 + 0.1 * np.random.standard_normal(1)),
            "bx": bf(1.0 + 0.1 * np.random.standard_normal(1))}


def reference(h, x2f, vu, w_f, b_f, bh, bx):
    h2f = (mxq(f64(h), 1, "e4m3") @ mxq(f64(w_f), 1, "e4m3").T) + f64(b_f)
    vuq = mxq(f64(vu), 2, "e4m3").transpose(1, 2, 0)
    ah = (mxq(f64(x2f).reshape(B, S, DS), 2, "e4m3").transpose(1, 0, 2) @ vuq).transpose(1, 2, 0)
    ax = (mxq(h2f.reshape(B, S, DS), 2, "e4m3").transpose(1, 0, 2) @ vuq).transpose(1, 2, 0)
    ah = np.maximum(ah + f64(bh), 0.0)
    ax = np.maximum(ax + f64(bx), 0.0)
    a2 = (ah + ax) ** 2
    return a2 / np.maximum(a2.sum(axis=1, keepdims=True), EPS)

@@ -1,0 +1,331 @@
+from contextlib import ExitStack
+
+import concourse.mybir as mybir
+from concourse.masks import make_identity
+
+F32 = mybir.dt.float32
+BF16 = mybir.dt.bfloat16
+U32 = mybir.dt.uint32
+U8 = mybir.dt.uint8
+FP8X4 = mybir.dt.float8_e4m3fn_x4
+ALU = mybir.AluOpType
+ACT = mybir.ActivationFunctionType
+
+P = 128
+ROWS = 4096
+FEATURES = 1024
+ROLES = 128
+EPS = 1e-12
+
+PACK = 4
+HALVES = 2
+PAIR = 2
+SPAN = P * PACK
+SPANS = FEATURES // SPAN
+ROW_WORDS = FEATURES // PAIR
+
+ROUND_TILES = 2
+ROUNDS = ROWS // (P * ROUND_TILES)
+ROW_BUFS = 6
+ROUND_COLS = ROUND_TILES * FEATURES
+SCORE_COLS = ROUND_TILES * SPANS * ROLES
+
+FLOPS = 2 * ROWS * FEATURES * FEATURES + 2 * 2 * ROWS * FEATURES * ROLES
+
+
+def tile_tpru_pa_t_kernel(tc, h, x2f, vu, w_f, b_f, bh, bx, out):
+    nc = tc.nc
+    with ExitStack() as ctx:
+        const = ctx.enter_context(tc.tile_pool(name="const", bufs=1))
+        rows_pool = ctx.enter_context(tc.tile_pool(name="rows", bufs=ROW_BUFS))
+        grouped_pool = ctx.enter_context(tc.tile_pool(name="grouped", bufs=2))
+        codes_pool = ctx.enter_context(tc.tile_pool(name="codes", bufs=2))
+        tail_pool = ctx.enter_context(tc.tile_pool(name="tail", bufs=3))
+        h2f_psum = ctx.enter_context(tc.psum_pool(name="h2f_psum", bufs=3))
+        turn_psum = ctx.enter_context(tc.psum_pool(name="turn_psum", bufs=5))
+        ctx.enter_context(tc.manual_schedule())
+
+        dram_rounds = {
+            "h": h.rearrange("(i p j) k -> i p (j k)", p=P, j=ROUND_TILES),
+            "x": x2f.rearrange("(i p j) k -> i p (j k)", p=P, j=ROUND_TILES),
+            "out": out.rearrange("(i p j) n s -> i p (j n s)", p=P, j=ROUND_TILES),
+        }
+
+        rows = {}
+        grouped = {}
+        codes = {}
+        scales = {}
+        scores = {}
+        tail = {}
+
+        def live(i):
+            return 0 <= i < ROUNDS
+
+        def load(operand, i):
+            if not live(i):
+                return
+            loaded = rows_pool.tile([P, ROUND_COLS], BF16, name=operand + "_rows")
+            nc.sync.dma_start(out=loaded[:], in_=dram_rounds[operand][i])
+            rows[operand, i] = loaded
+
+        def word_tiles(values, tiles):
+            return values[:].bitcast(F32).rearrange(
+                "p (j g r u) -> p j g r u", j=tiles, g=SPANS, r=P, u=HALVES
+            )
+
+        def flip_tile(row_words, grouped_words, copy):
+            flipped = turn_psum.tile([P, SPANS, HALVES, P], F32, tag="turn")
+            for g in range(SPANS):
+                for u in range(HALVES):
+                    span_words = row_words[:, g * HALVES * P : (g + 1) * HALVES * P]
+                    nc.tensor.transpose(
+                        flipped[:, g, u, :], span_words[:, u::HALVES], identity[:]
+                    )
+            copy(out=grouped_words, in_=flipped[:].rearrange("p g u r -> p g r u"))
+
+        identity = const.tile([P, P], F32)
+        make_identity(nc, identity[:])
+
+        vu_rows = const.tile([P, FEATURES], BF16)
+        nc.scalar.dma_start(out=vu_rows[:], in_=vu.rearrange("n s d -> n (s d)"))
+        bias = const.tile([P, SPANS * PACK], BF16)
+        nc.scalar.dma_start(
+            out=bias[:].rearrange("c (s t) -> c s t", t=PACK),
+            in_=b_f.rearrange("(s c t) -> c s t", s=SPANS, c=P, t=PACK),
+        )
+        bh_raw = const.tile([P, 1], BF16)
+        nc.scalar.dma_start(out=bh_raw[:], in_=bh.partition_broadcast(P))
+        bx_raw = const.tile([P, 1], BF16)
+        nc.scalar.dma_start(out=bx_raw[:], in_=bx.partition_broadcast(P))
+
+        w_rows = const.tile([P, SPANS * PACK * FEATURES], BF16)
+        w_slices = w_f.rearrange("(s c t) k -> s c (t k)", s=SPANS, c=P, t=PACK)
+        for m in range(SPANS * HALVES):
+            first = (m % HALVES) * PAIR * FEATURES
+            nc.sync.dma_start(
+                out=w_rows[:, m * PAIR * FEATURES : (m + 1) * PAIR * FEATURES],
+                in_=w_slices[m // HALVES][:, first : first + PAIR * FEATURES],
+            )
+        for i in range(ROW_BUFS):
+            load("h", i)
+            load("x", i - 1)
+
+        vu_grouped = const.tile([P, FEATURES], BF16, align_bytes=64)
+        vu_codes = const.tile([P, SPANS, ROLES], U32, align_bytes=64)
+        vu_scales = const.tile([P, SPANS, ROLES], U8, align_bytes=64)
+        flip_tile(vu_rows[:].bitcast(F32), word_tiles(vu_grouped, 1)[:, 0], nc.scalar.copy)
+        nc.vector.quantize_mx(
+            out=vu_codes[:].rearrange("d s n -> d (s n)").bitcast(FP8X4),
+            scales=vu_scales[:].rearrange("d s n -> d (s n)"),
+            in_=vu_grouped[:],
+        )
+
+        w_words = w_rows[:].bitcast(F32)
+        w_grouped = const.tile([P, SPANS * PACK * FEATURES], BF16, align_bytes=64)
+        w_grouped_words = word_tiles(w_grouped, SPANS * PACK)
+        w_codes = const.tile([P, SPANS, PACK, SPANS, P], U32, align_bytes=64)
+        w_scales = const.tile([P, SPANS, PACK, SPANS, P], U8, align_bytes=64)
+        for s in range(SPANS):
+            for t in range(PACK):
+                m = s * PACK + t
+                flip_tile(
+                    w_words[:, m * ROW_WORDS : (m + 1) * ROW_WORDS],
+                    w_grouped_words[:, m],
+                    nc.scalar.copy if t % 2 == 0 else nc.vector.tensor_copy,
+                )
+            nc.vector.quantize_mx(
+                out=w_codes[:, s].rearrange("k t g c -> k (t g c)").bitcast(FP8X4),
+                scales=w_scales[:, s].rearrange("k t g c -> k (t g c)"),
+                in_=w_grouped[:, s * PACK * FEATURES : (s + 1) * PACK * FEATURES],
+            )
+
+        bh_f32 = const.tile([P, 1], F32)
+        nc.vector.tensor_copy(out=bh_f32[:], in_=bh_raw[:])
+        bx_f32 = const.tile([P, 1], F32)
+        nc.vector.tensor_copy(out=bx_f32[:], in_=bx_raw[:])
+        score_bias = {"x": bh_f32, "h2f": bx_f32}
+
+        def flip(operand, i, j):
+            if not live(i):
+                return
+            if j == 0:
+                grouped[operand, i] = grouped_pool.tile(
+                    [P, ROUND_COLS], BF16, name=operand + "_grouped", align_bytes=64
+                )
+            flip_tile(
+                rows[operand, i][:].bitcast(F32)[:, j * ROW_WORDS : (j + 1) * ROW_WORDS],
+                word_tiles(grouped[operand, i], ROUND_TILES)[:, j],
+                nc.scalar.copy,
+            )
+            if j == ROUND_TILES - 1:
+                load(operand, i + ROW_BUFS if operand == "h" else i + ROW_BUFS - 1)
+
+        def quantise(operand, i):
+            if not live(i):
+                return
+            words = codes_pool.tile(
+                [P, ROUND_TILES, SPANS, P], U32, name=operand + "_codes", align_bytes=64
+            )
+            plane = codes_pool.tile(
+                [P, ROUND_TILES, SPANS, P], U8, name=operand + "_scales", align_bytes=64
+            )
+            nc.vector.quantize_mx(
+                out=words[:].rearrange("k j g r -> k (j g r)").bitcast(FP8X4),
+                scales=plane[:].rearrange("k j g r -> k (j g r)"),
+                in_=grouped[operand, i][:],
+            )
+            codes[operand, i] = words
+            scales[operand, i] = plane
+
+        def project(i, j, s):
+            if not live(i):
+                return
+            if (j, s) == (0, 0):
+                h2f_grouped = grouped_pool.tile([P, ROUND_COLS], BF16, align_bytes=64)
+                grouped["h2f", i] = h2f_grouped
+            sums = h2f_psum.tile([P, PACK, P], F32)
+            for t in range(PACK):
+                for g in range(SPANS):
+                    nc.tensor.matmul_mx(
+                        out=sums[:, t, :],
+                        lhsT=w_codes[:, s, t, g, :].bitcast(FP8X4),
+                        lhsT_scale=w_scales[:, s, t, g, :],
+                        rhs=codes["h", i][:, j, g, :].bitcast(FP8X4),
+                        rhs_scale=scales["h", i][:, j, g, :],
+                        start=(g == 0),
+                        stop=(g == SPANS - 1),
+                    )
+            nc.vector.tensor_tensor(
+                out=grouped["h2f", i][:].rearrange(
+                    "c (j s r t) -> c j s r t", j=ROUND_TILES, s=SPANS, r=P, t=PACK
+                )[:, j, s],
+                in0=sums[:].rearrange("c t r -> c r t"),
+                in1=bias[:, s * PACK : (s + 1) * PACK].unsqueeze(1).to_broadcast([P, P, PACK]),
+                op=ALU.add,
+            )
+
+        def score(i):
+            if not live(i):
+                return
+            for operand in ("x", "h2f"):
+                bank = turn_psum.tile(
+                    [P, ROUND_TILES, SPANS, ROLES], F32, name=operand + "_scores", tag="turn"
+                )
+                scores[operand, i] = bank
+                for j in range(ROUND_TILES):
+                    for s in range(SPANS):
+                        nc.tensor.matmul_mx(
+                            out=bank[:, j, s, :],
+                            lhsT=codes[operand, i][:, j, s, :].bitcast(FP8X4),
+                            lhsT_scale=scales[operand, i][:, j, s, :],
+                            rhs=vu_codes[:, s, :].bitcast(FP8X4),
+                            rhs_scale=vu_scales[:, s, :],
+                            start=True,
+                            stop=True,
+                        )
+
+        def relu(operand, i):
+            if not live(i):
+                return
+            kept = tail_pool.tile([P, SCORE_COLS], F32, name=operand + "_relu")
+            tail[operand, i] = kept
+            nc.scalar.activation(
+                out=kept[:],
+                in_=scores[operand, i][:].rearrange("r j s n -> r (j s n)"),
+                func=ACT.Relu,
+                bias=score_bias[operand][:, 0:1],
+                scale=1.0,
+            )
+
+        def add(helper, i):
+            if not live(i):
+                return
+            both = tail_pool.tile([P, SCORE_COLS], F32)
+            tail["both", i] = both
+            helper.tensor_tensor(
+                out=both[:], in0=tail["x", i][:], in1=tail["h2f", i][:], op=ALU.add
+            )
+
+        def square(i):
+            if not live(i):
+                return
+            a2 = tail_pool.tile([P, SCORE_COLS], F32)
+            totals = tail_pool.tile([P, ROUND_TILES * SPANS], F32)
+            tail["a2", i] = a2
+            tail["totals", i] = totals
+            for q in range(ROUND_TILES * SPANS):
+                nc.scalar.activation(
+                    out=a2[:, q * ROLES : (q + 1) * ROLES],
+                    in_=tail["both", i][:, q * ROLES : (q + 1) * ROLES],
+                    func=ACT.Square,
+                    accum_out=totals[:, q : q + 1],
+                )
+
+        def floor_totals(i):
+            if not live(i):
+                return
+            floored = tail_pool.tile([P, ROUND_TILES * SPANS], F32)
+            tail["floored", i] = floored
+            nc.vector.tensor_scalar_max(out=floored[:], in0=tail["totals", i][:], scalar1=EPS)
+
+        def invert_totals(i):
+            if not live(i):
+                return
+            inverse = tail_pool.tile([P, ROUND_TILES * SPANS], F32)
+            tail["inverse", i] = inverse
+            nc.vector.reciprocal(out=inverse[:], in_=tail["floored", i][:])
+
+        def normalise(helper, i):
+            if not live(i):
+                return
+            result = tail_pool.tile([P, SCORE_COLS], F32)
+            helper.tensor_tensor(
+                out=result[:].rearrange(
+                    "r (j n s) -> r j n s", j=ROUND_TILES, n=ROLES, s=SPANS
+                ),
+                in0=tail["a2", i][:].rearrange(
+                    "r (j s n) -> r j n s", j=ROUND_TILES, s=SPANS, n=ROLES
+                ),
+                in1=tail["inverse", i][:]
+                .rearrange("r (j s) -> r j s", s=SPANS)
+                .unsqueeze(2)
+                .to_broadcast([P, ROUND_TILES, ROLES, SPANS]),
+                op=ALU.mult,
+            )
+            nc.sync.dma_start(out=dram_rounds["out"][i], in_=result[:])
+
+        for k in range(-3, ROUNDS - 1):
+            add(nc.gpsimd, k - 1)
+            normalise(nc.gpsimd, k - 2)
+            square(k - 1)
+            for j in range(ROUND_TILES):
+                for s in range(SPANS):
+                    project(k + 1, j, s)
+            floor_totals(k - 1)
+            quantise("h", k + 2)
+            quantise("x", k + 1)
+            quantise("h2f", k + 1)
+            invert_totals(k - 1)
+            score(k)
+            relu("x", k)
+            relu("h2f", k)
+            for j in range(ROUND_TILES):
+                flip("h", k + 3, j)
+            for j in range(ROUND_TILES):
+                flip("x", k + 2, j)
+
+        last = ROUNDS - 1
+        score(last)
+        relu("x", last)
+        relu("h2f", last)
+        add(nc.vector, last - 1)
+        normalise(nc.vector, last - 2)
+        square(last - 1)
+        add(nc.vector, last)
+        floor_totals(last - 1)
+        square(last)
+        invert_totals(last - 1)
+        normalise(nc.vector, last - 1)
+        floor_totals(last)
+        invert_totals(last)
+        normalise(nc.vector, last)

@@ -28,7 +28,8 @@ ROUND_TILES = 2
 ROUNDS = ROWS // (P * ROUND_TILES)
 ROW_BUFS = 6
 ROUND_COLS = ROUND_TILES * FEATURES
-SCORE_COLS = ROUND_TILES * SPANS * ROLES
+TILE_SCORES = SPANS * ROLES
+SCORE_COLS = ROUND_TILES * TILE_SCORES
 
 FLOPS = 2 * ROWS * FEATURES * FEATURES + 2 * 2 * ROWS * FEATURES * ROLES
 
@@ -38,6 +39,7 @@ def tile_tpru_pa_t_kernel(tc, h, x2f, vu, w_f, b_f, bh, bx, out):
     with ExitStack() as ctx:
         const = ctx.enter_context(tc.tile_pool(name="const", bufs=1))
         rows_pool = ctx.enter_context(tc.tile_pool(name="rows", bufs=ROW_BUFS))
+        dealt_pool = ctx.enter_context(tc.tile_pool(name="dealt", bufs=2))
         grouped_pool = ctx.enter_context(tc.tile_pool(name="grouped", bufs=2))
         codes_pool = ctx.enter_context(tc.tile_pool(name="codes", bufs=2))
         tail_pool = ctx.enter_context(tc.tile_pool(name="tail", bufs=3))
@@ -52,6 +54,7 @@ def tile_tpru_pa_t_kernel(tc, h, x2f, vu, w_f, b_f, bh, bx, out):
         }
 
         rows = {}
+        dealt = {}
         grouped = {}
         codes = {}
         scales = {}
@@ -73,79 +76,89 @@ def tile_tpru_pa_t_kernel(tc, h, x2f, vu, w_f, b_f, bh, bx, out):
                 "p (j g r u) -> p j g r u", j=tiles, g=SPANS, r=P, u=HALVES
             )
 
+        def deal(operand, i, j, copy):
+            if not live(i):
+                return
+            sorted_words = dealt_pool.tile(
+                [P, SPANS, HALVES, P], F32, name=operand + "_dealt" + str(j)
+            )
+            copy(
+                out=sorted_words[:],
+                in_=loaded_words(rows[operand, i], j),
+            )
+            dealt[operand, i, j] = sorted_words
+
+        def loaded_words(values, j):
+            return values[:].bitcast(F32)[:, j * ROW_WORDS : (j + 1) * ROW_WORDS].rearrange(
+                "r (g p u) -> r g u p", g=SPANS, u=HALVES
+            )
+
         def flip_tile(row_words, grouped_words, copy):
             flipped = turn_psum.tile([P, SPANS, HALVES, P], F32, tag="turn")
             for g in range(SPANS):
                 for u in range(HALVES):
-                    span_words = row_words[:, g * HALVES * P : (g + 1) * HALVES * P]
-                    nc.tensor.transpose(
-                        flipped[:, g, u, :], span_words[:, u::HALVES], identity[:]
-                    )
+                    nc.tensor.transpose(flipped[:, g, u, :], row_words[:, g, u, :], identity[:])
             copy(out=grouped_words, in_=flipped[:].rearrange("p g u r -> p g r u"))
 
         identity = const.tile([P, P], F32)
         make_identity(nc, identity[:])
 
-        vu_rows = const.tile([P, FEATURES], BF16)
-        nc.scalar.dma_start(out=vu_rows[:], in_=vu.rearrange("n s d -> n (s d)"))
+        w_rows = const.tile([P, SPANS * PACK * FEATURES], BF16)
+        w_tiles = w_f.rearrange("(s c t) k -> s t c k", s=SPANS, c=P, t=PACK)
+        for s in range(SPANS):
+            for t in range(PACK):
+                m = s * PACK + t
+                nc.sync.dma_start(
+                    out=w_rows[:, m * FEATURES : (m + 1) * FEATURES], in_=w_tiles[s][t]
+                )
         bias = const.tile([P, SPANS * PACK], BF16)
-        nc.scalar.dma_start(
+        nc.gpsimd.dma_start(
             out=bias[:].rearrange("c (s t) -> c s t", t=PACK),
             in_=b_f.rearrange("(s c t) -> c s t", s=SPANS, c=P, t=PACK),
         )
         bh_raw = const.tile([P, 1], BF16)
-        nc.scalar.dma_start(out=bh_raw[:], in_=bh.partition_broadcast(P))
+        nc.gpsimd.dma_start(out=bh_raw[:], in_=bh.partition_broadcast(P))
         bx_raw = const.tile([P, 1], BF16)
-        nc.scalar.dma_start(out=bx_raw[:], in_=bx.partition_broadcast(P))
+        nc.gpsimd.dma_start(out=bx_raw[:], in_=bx.partition_broadcast(P))
 
-        w_rows = const.tile([P, SPANS * PACK * FEATURES], BF16)
-        w_slices = w_f.rearrange("(s c t) k -> s c (t k)", s=SPANS, c=P, t=PACK)
-        for m in range(SPANS * HALVES):
-            first = (m % HALVES) * PAIR * FEATURES
-            nc.sync.dma_start(
-                out=w_rows[:, m * PAIR * FEATURES : (m + 1) * PAIR * FEATURES],
-                in_=w_slices[m // HALVES][:, first : first + PAIR * FEATURES],
-            )
-        for i in range(ROW_BUFS):
+        load("h", 0)
+        vu_rows = const.tile([P, FEATURES], BF16)
+        nc.sync.dma_start(out=vu_rows[:], in_=vu.rearrange("n s d -> n (s d)"))
+        for i in range(1, ROW_BUFS):
             load("h", i)
             load("x", i - 1)
+        load("x", ROW_BUFS - 1)
 
-        vu_grouped = const.tile([P, FEATURES], BF16, align_bytes=64)
-        vu_codes = const.tile([P, SPANS, ROLES], U32, align_bytes=64)
-        vu_scales = const.tile([P, SPANS, ROLES], U8, align_bytes=64)
-        flip_tile(vu_rows[:].bitcast(F32), word_tiles(vu_grouped, 1)[:, 0], nc.scalar.copy)
-        nc.vector.quantize_mx(
-            out=vu_codes[:].rearrange("d s n -> d (s n)").bitcast(FP8X4),
-            scales=vu_scales[:].rearrange("d s n -> d (s n)"),
-            in_=vu_grouped[:],
-        )
-
-        w_words = w_rows[:].bitcast(F32)
         w_grouped = const.tile([P, SPANS * PACK * FEATURES], BF16, align_bytes=64)
         w_grouped_words = word_tiles(w_grouped, SPANS * PACK)
         w_codes = const.tile([P, SPANS, PACK, SPANS, P], U32, align_bytes=64)
         w_scales = const.tile([P, SPANS, PACK, SPANS, P], U8, align_bytes=64)
+
+        def quantise_w(s, t):
+            m = s * PACK + t
+            nc.vector.quantize_mx(
+                out=w_codes[:, s, t : t + 2].rearrange("k t g c -> k (t g c)").bitcast(FP8X4),
+                scales=w_scales[:, s, t : t + 2].rearrange("k t g c -> k (t g c)"),
+                in_=w_grouped[:, m * FEATURES : (m + 2) * FEATURES],
+            )
+
         for s in range(SPANS):
             for t in range(PACK):
                 m = s * PACK + t
                 flip_tile(
-                    w_words[:, m * ROW_WORDS : (m + 1) * ROW_WORDS],
+                    loaded_words(w_rows, m),
                     w_grouped_words[:, m],
                     nc.scalar.copy if t % 2 == 0 else nc.vector.tensor_copy,
                 )
-            nc.vector.quantize_mx(
-                out=w_codes[:, s].rearrange("k t g c -> k (t g c)").bitcast(FP8X4),
-                scales=w_scales[:, s].rearrange("k t g c -> k (t g c)"),
-                in_=w_grouped[:, s * PACK * FEATURES : (s + 1) * PACK * FEATURES],
-            )
+                if t == 3:
+                    quantise_w(s, 0)
+                elif t == 1 and s > 0:
+                    quantise_w(s - 1, 2)
 
-        bh_f32 = const.tile([P, 1], F32)
-        nc.vector.tensor_copy(out=bh_f32[:], in_=bh_raw[:])
-        bx_f32 = const.tile([P, 1], F32)
-        nc.vector.tensor_copy(out=bx_f32[:], in_=bx_raw[:])
-        score_bias = {"x": bh_f32, "h2f": bx_f32}
+        score_bias = {"x": bh_raw, "h2f": bx_raw}
+        minus_bx = const.tile([P, 1], F32)
 
-        def flip(operand, i, j):
+        def flip(operand, i, j, copy):
             if not live(i):
                 return
             if j == 0:
@@ -153,26 +166,32 @@ def tile_tpru_pa_t_kernel(tc, h, x2f, vu, w_f, b_f, bh, bx, out):
                     [P, ROUND_COLS], BF16, name=operand + "_grouped", align_bytes=64
                 )
             flip_tile(
-                rows[operand, i][:].bitcast(F32)[:, j * ROW_WORDS : (j + 1) * ROW_WORDS],
+                dealt[operand, i, j]
+                if (operand, i, j) in dealt
+                else loaded_words(rows[operand, i], j),
                 word_tiles(grouped[operand, i], ROUND_TILES)[:, j],
-                nc.scalar.copy,
+                copy,
             )
             if j == ROUND_TILES - 1:
-                load(operand, i + ROW_BUFS if operand == "h" else i + ROW_BUFS - 1)
+                load(operand, i + ROW_BUFS)
 
-        def quantise(operand, i):
+        def quantise(operand, i, lo=0, hi=ROUND_TILES):
             if not live(i):
                 return
+            if lo == 0:
+                new_codes(operand, i)
+            nc.vector.quantize_mx(
+                out=codes[operand, i][:, lo:hi].rearrange("k j g r -> k (j g r)").bitcast(FP8X4),
+                scales=scales[operand, i][:, lo:hi].rearrange("k j g r -> k (j g r)"),
+                in_=grouped[operand, i][:, lo * FEATURES : hi * FEATURES],
+            )
+
+        def new_codes(operand, i):
             words = codes_pool.tile(
                 [P, ROUND_TILES, SPANS, P], U32, name=operand + "_codes", align_bytes=64
             )
             plane = codes_pool.tile(
                 [P, ROUND_TILES, SPANS, P], U8, name=operand + "_scales", align_bytes=64
-            )
-            nc.vector.quantize_mx(
-                out=words[:].rearrange("k j g r -> k (j g r)").bitcast(FP8X4),
-                scales=plane[:].rearrange("k j g r -> k (j g r)"),
-                in_=grouped[operand, i][:],
             )
             codes[operand, i] = words
             scales[operand, i] = plane
@@ -204,25 +223,25 @@ def tile_tpru_pa_t_kernel(tc, h, x2f, vu, w_f, b_f, bh, bx, out):
                 op=ALU.add,
             )
 
-        def score(i):
+        def score(operand, i, lo=0, hi=ROUND_TILES):
             if not live(i):
                 return
-            for operand in ("x", "h2f"):
+            if lo == 0:
                 bank = turn_psum.tile(
                     [P, ROUND_TILES, SPANS, ROLES], F32, name=operand + "_scores", tag="turn"
                 )
                 scores[operand, i] = bank
-                for j in range(ROUND_TILES):
-                    for s in range(SPANS):
-                        nc.tensor.matmul_mx(
-                            out=bank[:, j, s, :],
-                            lhsT=codes[operand, i][:, j, s, :].bitcast(FP8X4),
-                            lhsT_scale=scales[operand, i][:, j, s, :],
-                            rhs=vu_codes[:, s, :].bitcast(FP8X4),
-                            rhs_scale=vu_scales[:, s, :],
-                            start=True,
-                            stop=True,
-                        )
+            for j in range(lo, hi):
+                for s in range(SPANS):
+                    nc.tensor.matmul_mx(
+                        out=scores[operand, i][:, j, s, :],
+                        lhsT=codes[operand, i][:, j, s, :].bitcast(FP8X4),
+                        lhsT_scale=scales[operand, i][:, j, s, :],
+                        rhs=vu_codes[:, s, :].bitcast(FP8X4),
+                        rhs_scale=vu_scales[:, s, :],
+                        start=True,
+                        stop=True,
+                    )
 
         def relu(operand, i):
             if not live(i):
@@ -246,58 +265,98 @@ def tile_tpru_pa_t_kernel(tc, h, x2f, vu, w_f, b_f, bh, bx, out):
                 out=both[:], in0=tail["x", i][:], in1=tail["h2f", i][:], op=ALU.add
             )
 
-        def square(i):
+        def join(i, lo, hi):
+            if lo == 0:
+                both = tail_pool.tile([P, SCORE_COLS], F32)
+                tail["both", i] = both
+            nc.vector.scalar_tensor_tensor(
+                out=tail["both", i][:, lo * TILE_SCORES : hi * TILE_SCORES],
+                in0=scores["h2f", i][:, lo:hi].rearrange("r j s n -> r (j s n)"),
+                scalar=minus_bx[:, 0:1],
+                in1=tail["x", i][:, lo * TILE_SCORES : hi * TILE_SCORES],
+                op0=ALU.max,
+                op1=ALU.add,
+            )
+
+        def square(i, lo=0, hi=ROUND_TILES, bias=0.0):
             if not live(i):
                 return
-            a2 = tail_pool.tile([P, SCORE_COLS], F32)
-            totals = tail_pool.tile([P, ROUND_TILES * SPANS], F32)
-            tail["a2", i] = a2
-            tail["totals", i] = totals
-            for q in range(ROUND_TILES * SPANS):
+            if lo == 0:
+                a2 = tail_pool.tile([P, SCORE_COLS], F32)
+                totals = tail_pool.tile([P, ROUND_TILES * SPANS], F32)
+                tail["a2", i] = a2
+                tail["totals", i] = totals
+            for q in range(lo * SPANS, hi * SPANS):
                 nc.scalar.activation(
-                    out=a2[:, q * ROLES : (q + 1) * ROLES],
+                    out=tail["a2", i][:, q * ROLES : (q + 1) * ROLES],
                     in_=tail["both", i][:, q * ROLES : (q + 1) * ROLES],
                     func=ACT.Square,
-                    accum_out=totals[:, q : q + 1],
+                    bias=bias,
+                    scale=1.0,
+                    accum_out=tail["totals", i][:, q : q + 1],
                 )
 
-        def floor_totals(i):
+        def floor_totals(i, lo=0, hi=ROUND_TILES):
             if not live(i):
                 return
-            floored = tail_pool.tile([P, ROUND_TILES * SPANS], F32)
-            tail["floored", i] = floored
-            nc.vector.tensor_scalar_max(out=floored[:], in0=tail["totals", i][:], scalar1=EPS)
+            if lo == 0:
+                floored = tail_pool.tile([P, ROUND_TILES * SPANS], F32)
+                tail["floored", i] = floored
+            nc.vector.tensor_scalar_max(
+                out=tail["floored", i][:, lo * SPANS : hi * SPANS],
+                in0=tail["totals", i][:, lo * SPANS : hi * SPANS],
+                scalar1=EPS,
+            )
 
-        def invert_totals(i):
+        def invert_totals(i, lo=0, hi=ROUND_TILES):
             if not live(i):
                 return
-            inverse = tail_pool.tile([P, ROUND_TILES * SPANS], F32)
-            tail["inverse", i] = inverse
-            nc.vector.reciprocal(out=inverse[:], in_=tail["floored", i][:])
+            if lo == 0:
+                inverse = tail_pool.tile([P, ROUND_TILES * SPANS], F32)
+                tail["inverse", i] = inverse
+            nc.vector.reciprocal(
+                out=tail["inverse", i][:, lo * SPANS : hi * SPANS],
+                in_=tail["floored", i][:, lo * SPANS : hi * SPANS],
+            )
 
-        def normalise(helper, i):
+        def normalise(helper, i, lo=0, hi=ROUND_TILES):
             if not live(i):
                 return
-            result = tail_pool.tile([P, SCORE_COLS], F32)
+            if lo == 0:
+                result = tail_pool.tile([P, SCORE_COLS], F32)
+                tail["result", i] = result
+            cols = slice(lo * TILE_SCORES, hi * TILE_SCORES)
             helper.tensor_tensor(
-                out=result[:].rearrange(
-                    "r (j n s) -> r j n s", j=ROUND_TILES, n=ROLES, s=SPANS
+                out=tail["result", i][:, cols].rearrange(
+                    "r (j n s) -> r j n s", j=hi - lo, n=ROLES, s=SPANS
                 ),
-                in0=tail["a2", i][:].rearrange(
-                    "r (j s n) -> r j n s", j=ROUND_TILES, s=SPANS, n=ROLES
+                in0=tail["a2", i][:, cols].rearrange(
+                    "r (j s n) -> r j n s", j=hi - lo, s=SPANS, n=ROLES
                 ),
-                in1=tail["inverse", i][:]
+                in1=tail["inverse", i][:, lo * SPANS : hi * SPANS]
                 .rearrange("r (j s) -> r j s", s=SPANS)
                 .unsqueeze(2)
-                .to_broadcast([P, ROUND_TILES, ROLES, SPANS]),
+                .to_broadcast([P, hi - lo, ROLES, SPANS]),
                 op=ALU.mult,
             )
-            nc.sync.dma_start(out=dram_rounds["out"][i], in_=result[:])
+            nc.sync.dma_start(out=dram_rounds["out"][i][:, cols], in_=tail["result", i][:, cols])
 
-        for k in range(-3, ROUNDS - 1):
+        flip("h", 0, 0, nc.scalar.copy)
+        flip("h", 0, 1, nc.vector.tensor_copy)
+        quantise_w(SPANS - 1, 2)
+
+        vu_grouped = const.tile([P, FEATURES], BF16, align_bytes=64)
+        vu_codes = const.tile([P, SPANS, ROLES], U32, align_bytes=64)
+        vu_scales = const.tile([P, SPANS, ROLES], U8, align_bytes=64)
+        flip_tile(loaded_words(vu_rows, 0), word_tiles(vu_grouped, 1)[:, 0], nc.scalar.copy)
+
+        for k in range(-2, ROUNDS - 2):
             add(nc.gpsimd, k - 1)
             normalise(nc.gpsimd, k - 2)
             square(k - 1)
+            if k >= 0:
+                deal("h", k + 4, 0, nc.scalar.copy)
+                deal("x", k + 3, 0, nc.vector.tensor_copy)
             for j in range(ROUND_TILES):
                 for s in range(SPANS):
                     project(k + 1, j, s)
@@ -305,27 +364,57 @@ def tile_tpru_pa_t_kernel(tc, h, x2f, vu, w_f, b_f, bh, bx, out):
             quantise("h", k + 2)
             quantise("x", k + 1)
             quantise("h2f", k + 1)
+            if k == -1:
+                nc.vector.quantize_mx(
+                    out=vu_codes[:].rearrange("d s n -> d (s n)").bitcast(FP8X4),
+                    scales=vu_scales[:].rearrange("d s n -> d (s n)"),
+                    in_=vu_grouped[:],
+                )
             invert_totals(k - 1)
-            score(k)
+            score("x", k)
+            score("h2f", k)
             relu("x", k)
             relu("h2f", k)
             for j in range(ROUND_TILES):
-                flip("h", k + 3, j)
+                flip("h", k + 3, j, nc.scalar.copy)
             for j in range(ROUND_TILES):
-                flip("x", k + 2, j)
+                flip("x", k + 2, j, nc.scalar.copy)
 
         last = ROUNDS - 1
-        score(last)
+        add(nc.gpsimd, last - 2)
+        normalise(nc.gpsimd, last - 3)
+        square(last - 2)
+        score("x", last - 1)
+        score("h2f", last - 1)
+        quantise("x", last)
+        nc.vector.tensor_scalar_mul(out=minus_bx[:], in0=bx_raw[:], scalar1=-1.0)
+        relu("x", last - 1)
+        relu("h2f", last - 1)
+        add(nc.gpsimd, last - 1)
+        floor_totals(last - 2)
+        project(last, 0, 0)
+        invert_totals(last - 2)
+        project(last, 0, 1)
+        score("x", last)
         relu("x", last)
-        relu("h2f", last)
-        add(nc.vector, last - 1)
-        normalise(nc.vector, last - 2)
+        project(last, 1, 0)
+        quantise("h2f", last, 0, 1)
+        project(last, 1, 1)
+        score("h2f", last, 0, 1)
+        normalise(nc.gpsimd, last - 2)
         square(last - 1)
-        add(nc.vector, last)
+        join(last, 0, 1)
+        quantise("h2f", last, 1, 2)
         floor_totals(last - 1)
-        square(last)
+        score("h2f", last, 1, 2)
+        square(last, 0, 1, bx_raw[:, 0:1])
         invert_totals(last - 1)
-        normalise(nc.vector, last - 1)
-        floor_totals(last)
-        invert_totals(last)
-        normalise(nc.vector, last)
+        join(last, 1, 2)
+        normalise(nc.gpsimd, last - 1)
+        floor_totals(last, 0, 1)
+        square(last, 1, 2, bx_raw[:, 0:1])
+        invert_totals(last, 0, 1)
+        normalise(nc.vector, last, 0, 1)
+        floor_totals(last, 1, 2)
+        invert_totals(last, 1, 2)
+        normalise(nc.vector, last, 1, 2)

@@ -42,7 +42,7 @@ def tile_tpru_pa_t_kernel(tc, h, x2f, vu, w_f, b_f, bh, bx, out):
         dealt_pool = ctx.enter_context(tc.tile_pool(name="dealt", bufs=2))
         grouped_pool = ctx.enter_context(tc.tile_pool(name="grouped", bufs=2))
         codes_pool = ctx.enter_context(tc.tile_pool(name="codes", bufs=2))
-        tail_pool = ctx.enter_context(tc.tile_pool(name="tail", bufs=3))
+        tail_pool = ctx.enter_context(tc.tile_pool(name="tail", bufs=4))
         h2f_psum = ctx.enter_context(tc.psum_pool(name="h2f_psum", bufs=3))
         turn_psum = ctx.enter_context(tc.psum_pool(name="turn_psum", bufs=5))
         ctx.enter_context(tc.manual_schedule())
@@ -351,18 +351,19 @@ def tile_tpru_pa_t_kernel(tc, h, x2f, vu, w_f, b_f, bh, bx, out):
         flip_tile(loaded_words(vu_rows, 0), word_tiles(vu_grouped, 1)[:, 0], nc.scalar.copy)
 
         for k in range(-2, ROUNDS - 2):
+            normalise(nc.gpsimd, k - 3)
             add(nc.gpsimd, k - 1)
-            normalise(nc.gpsimd, k - 2)
-            square(k - 1)
+            square(k - 2)
             if k >= 0:
                 deal("h", k + 4, 0, nc.scalar.copy)
-                deal("x", k + 3, 0, nc.vector.tensor_copy)
             for j in range(ROUND_TILES):
                 for s in range(SPANS):
                     project(k + 1, j, s)
-            floor_totals(k - 1)
+            floor_totals(k - 2)
             quantise("h", k + 2)
             quantise("x", k + 1)
+            if k >= 0:
+                deal("x", k + 3, 0, nc.vector.tensor_copy)
             quantise("h2f", k + 1)
             if k == -1:
                 nc.vector.quantize_mx(
@@ -370,7 +371,7 @@ def tile_tpru_pa_t_kernel(tc, h, x2f, vu, w_f, b_f, bh, bx, out):
                     scales=vu_scales[:].rearrange("d s n -> d (s n)"),
                     in_=vu_grouped[:],
                 )
-            invert_totals(k - 1)
+            invert_totals(k - 2)
             score("x", k)
             score("h2f", k)
             relu("x", k)
@@ -381,38 +382,42 @@ def tile_tpru_pa_t_kernel(tc, h, x2f, vu, w_f, b_f, bh, bx, out):
                 flip("x", k + 2, j, nc.scalar.copy)
 
         last = ROUNDS - 1
+        square_bias = bx_raw[:, 0:1]
+        normalise(nc.gpsimd, last - 4)
         add(nc.gpsimd, last - 2)
-        normalise(nc.gpsimd, last - 3)
-        square(last - 2)
+        square(last - 3)
         score("x", last - 1)
         score("h2f", last - 1)
+        relu("x", last - 1)
         quantise("x", last)
         nc.vector.tensor_scalar_mul(out=minus_bx[:], in0=bx_raw[:], scalar1=-1.0)
-        relu("x", last - 1)
-        relu("h2f", last - 1)
-        add(nc.gpsimd, last - 1)
-        floor_totals(last - 2)
+        floor_totals(last - 3)
         project(last, 0, 0)
-        invert_totals(last - 2)
+        invert_totals(last - 3)
+        normalise(nc.gpsimd, last - 3)
         project(last, 0, 1)
+        square(last - 2)
         score("x", last)
         relu("x", last)
+        join(last - 1, 0, ROUND_TILES)
+        floor_totals(last - 2)
         project(last, 1, 0)
+        square(last - 1, 0, ROUND_TILES, square_bias)
         quantise("h2f", last, 0, 1)
+        invert_totals(last - 2)
+        normalise(nc.gpsimd, last - 2)
         project(last, 1, 1)
         score("h2f", last, 0, 1)
-        normalise(nc.gpsimd, last - 2)
-        square(last - 1)
+        floor_totals(last - 1)
         join(last, 0, 1)
         quantise("h2f", last, 1, 2)
-        floor_totals(last - 1)
-        score("h2f", last, 1, 2)
-        square(last, 0, 1, bx_raw[:, 0:1])
         invert_totals(last - 1)
+        score("h2f", last, 1, 2)
+        square(last, 0, 1, square_bias)
+        normalise(nc.vector, last - 1)
         join(last, 1, 2)
-        normalise(nc.gpsimd, last - 1)
         floor_totals(last, 0, 1)
-        square(last, 1, 2, bx_raw[:, 0:1])
+        square(last, 1, 2, square_bias)
         invert_totals(last, 0, 1)
         normalise(nc.vector, last, 0, 1)
         floor_totals(last, 1, 2)

@@ -42,7 +42,7 @@ def tile_tpru_pa_t_kernel(tc, h, x2f, vu, w_f, b_f, bh, bx, out):
         dealt_pool = ctx.enter_context(tc.tile_pool(name="dealt", bufs=2))
         grouped_pool = ctx.enter_context(tc.tile_pool(name="grouped", bufs=2))
         codes_pool = ctx.enter_context(tc.tile_pool(name="codes", bufs=2))
-        tail_pool = ctx.enter_context(tc.tile_pool(name="tail", bufs=4))
+        tail_pool = ctx.enter_context(tc.tile_pool(name="tail", bufs=3))
         h2f_psum = ctx.enter_context(tc.psum_pool(name="h2f_psum", bufs=3))
         turn_psum = ctx.enter_context(tc.psum_pool(name="turn_psum", bufs=5))
         ctx.enter_context(tc.manual_schedule())
@@ -155,7 +155,6 @@ def tile_tpru_pa_t_kernel(tc, h, x2f, vu, w_f, b_f, bh, bx, out):
                 elif t == 1 and s > 0:
                     quantise_w(s - 1, 2)
 
-        score_bias = {"x": bh_raw, "h2f": bx_raw}
         minus_bx = const.tile([P, 1], F32)
 
         def flip(operand, i, j, copy):
@@ -243,29 +242,22 @@ def tile_tpru_pa_t_kernel(tc, h, x2f, vu, w_f, b_f, bh, bx, out):
                         stop=True,
                     )
 
-        def relu(operand, i):
+        def relu(i):
             if not live(i):
                 return
-            kept = tail_pool.tile([P, SCORE_COLS], F32, name=operand + "_relu")
-            tail[operand, i] = kept
+            ah = tail_pool.tile([P, SCORE_COLS], F32)
+            tail["ah", i] = ah
             nc.scalar.activation(
-                out=kept[:],
-                in_=scores[operand, i][:].rearrange("r j s n -> r (j s n)"),
+                out=ah[:],
+                in_=scores["x", i][:].rearrange("r j s n -> r (j s n)"),
                 func=ACT.Relu,
-                bias=score_bias[operand][:, 0:1],
+                bias=bh_raw[:, 0:1],
                 scale=1.0,
             )
 
-        def add(helper, i):
+        def join(i, lo=0, hi=ROUND_TILES):
             if not live(i):
                 return
-            both = tail_pool.tile([P, SCORE_COLS], F32)
-            tail["both", i] = both
-            helper.tensor_tensor(
-                out=both[:], in0=tail["x", i][:], in1=tail["h2f", i][:], op=ALU.add
-            )
-
-        def join(i, lo, hi):
             if lo == 0:
                 both = tail_pool.tile([P, SCORE_COLS], F32)
                 tail["both", i] = both
@@ -273,12 +265,12 @@ def tile_tpru_pa_t_kernel(tc, h, x2f, vu, w_f, b_f, bh, bx, out):
                 out=tail["both", i][:, lo * TILE_SCORES : hi * TILE_SCORES],
                 in0=scores["h2f", i][:, lo:hi].rearrange("r j s n -> r (j s n)"),
                 scalar=minus_bx[:, 0:1],
-                in1=tail["x", i][:, lo * TILE_SCORES : hi * TILE_SCORES],
+                in1=tail["ah", i][:, lo * TILE_SCORES : hi * TILE_SCORES],
                 op0=ALU.max,
                 op1=ALU.add,
             )
 
-        def square(i, lo=0, hi=ROUND_TILES, bias=0.0):
+        def square(i, lo=0, hi=ROUND_TILES):
             if not live(i):
                 return
             if lo == 0:
@@ -291,7 +283,7 @@ def tile_tpru_pa_t_kernel(tc, h, x2f, vu, w_f, b_f, bh, bx, out):
                     out=tail["a2", i][:, q * ROLES : (q + 1) * ROLES],
                     in_=tail["both", i][:, q * ROLES : (q + 1) * ROLES],
                     func=ACT.Square,
-                    bias=bias,
+                    bias=bx_raw[:, 0:1],
                     scale=1.0,
                     accum_out=tail["totals", i][:, q : q + 1],
                 )
@@ -344,6 +336,7 @@ def tile_tpru_pa_t_kernel(tc, h, x2f, vu, w_f, b_f, bh, bx, out):
         flip("h", 0, 0, nc.scalar.copy)
         flip("h", 0, 1, nc.vector.tensor_copy)
         quantise_w(SPANS - 1, 2)
+        nc.vector.tensor_scalar_mul(out=minus_bx[:], in0=bx_raw[:], scalar1=-1.0)
 
         vu_grouped = const.tile([P, FEATURES], BF16, align_bytes=64)
         vu_codes = const.tile([P, SPANS, ROLES], U32, align_bytes=64)
@@ -351,19 +344,17 @@ def tile_tpru_pa_t_kernel(tc, h, x2f, vu, w_f, b_f, bh, bx, out):
         flip_tile(loaded_words(vu_rows, 0), word_tiles(vu_grouped, 1)[:, 0], nc.scalar.copy)
 
         for k in range(-2, ROUNDS - 2):
-            normalise(nc.gpsimd, k - 3)
-            add(nc.gpsimd, k - 1)
-            square(k - 2)
+            normalise(nc.gpsimd, k - 2)
+            square(k - 1)
             if k >= 0:
                 deal("h", k + 4, 0, nc.scalar.copy)
+                deal("x", k + 3, 0, nc.scalar.copy)
             for j in range(ROUND_TILES):
                 for s in range(SPANS):
                     project(k + 1, j, s)
-            floor_totals(k - 2)
             quantise("h", k + 2)
+            floor_totals(k - 1)
             quantise("x", k + 1)
-            if k >= 0:
-                deal("x", k + 3, 0, nc.vector.tensor_copy)
             quantise("h2f", k + 1)
             if k == -1:
                 nc.vector.quantize_mx(
@@ -371,41 +362,34 @@ def tile_tpru_pa_t_kernel(tc, h, x2f, vu, w_f, b_f, bh, bx, out):
                     scales=vu_scales[:].rearrange("d s n -> d (s n)"),
                     in_=vu_grouped[:],
                 )
-            invert_totals(k - 2)
+            invert_totals(k - 1)
             score("x", k)
             score("h2f", k)
-            relu("x", k)
-            relu("h2f", k)
+            relu(k)
+            join(k)
             for j in range(ROUND_TILES):
                 flip("h", k + 3, j, nc.scalar.copy)
             for j in range(ROUND_TILES):
                 flip("x", k + 2, j, nc.scalar.copy)
 
         last = ROUNDS - 1
-        square_bias = bx_raw[:, 0:1]
-        normalise(nc.gpsimd, last - 4)
-        add(nc.gpsimd, last - 2)
-        square(last - 3)
+        normalise(nc.gpsimd, last - 3)
+        square(last - 2)
         score("x", last - 1)
         score("h2f", last - 1)
-        relu("x", last - 1)
+        relu(last - 1)
         quantise("x", last)
-        nc.vector.tensor_scalar_mul(out=minus_bx[:], in0=bx_raw[:], scalar1=-1.0)
-        floor_totals(last - 3)
-        project(last, 0, 0)
-        invert_totals(last - 3)
-        normalise(nc.gpsimd, last - 3)
-        project(last, 0, 1)
-        square(last - 2)
-        score("x", last)
-        relu("x", last)
-        join(last - 1, 0, ROUND_TILES)
         floor_totals(last - 2)
-        project(last, 1, 0)
-        square(last - 1, 0, ROUND_TILES, square_bias)
-        quantise("h2f", last, 0, 1)
+        project(last, 0, 0)
         invert_totals(last - 2)
         normalise(nc.gpsimd, last - 2)
+        project(last, 0, 1)
+        score("x", last)
+        relu(last)
+        join(last - 1)
+        project(last, 1, 0)
+        square(last - 1)
+        quantise("h2f", last, 0, 1)
         project(last, 1, 1)
         score("h2f", last, 0, 1)
         floor_totals(last - 1)
@@ -413,11 +397,11 @@ def tile_tpru_pa_t_kernel(tc, h, x2f, vu, w_f, b_f, bh, bx, out):
         quantise("h2f", last, 1, 2)
         invert_totals(last - 1)
         score("h2f", last, 1, 2)
-        square(last, 0, 1, square_bias)
+        square(last, 0, 1)
         normalise(nc.vector, last - 1)
         join(last, 1, 2)
         floor_totals(last, 0, 1)
-        square(last, 1, 2, square_bias)
+        square(last, 1, 2)
         invert_totals(last, 0, 1)
         normalise(nc.vector, last, 0, 1)
         floor_totals(last, 1, 2)

@@ -336,7 +336,6 @@ def tile_tpru_pa_t_kernel(tc, h, x2f, vu, w_f, b_f, bh, bx, out):
         flip("h", 0, 0, nc.scalar.copy)
         flip("h", 0, 1, nc.vector.tensor_copy)
         quantise_w(SPANS - 1, 2)
-        nc.vector.tensor_scalar_mul(out=minus_bx[:], in0=bx_raw[:], scalar1=-1.0)
 
         vu_grouped = const.tile([P, FEATURES], BF16, align_bytes=64)
         vu_codes = const.tile([P, SPANS, ROLES], U32, align_bytes=64)
@@ -349,6 +348,8 @@ def tile_tpru_pa_t_kernel(tc, h, x2f, vu, w_f, b_f, bh, bx, out):
             if k >= 0:
                 deal("h", k + 4, 0, nc.scalar.copy)
                 deal("x", k + 3, 0, nc.scalar.copy)
+                deal("h", k + 4, 1, nc.gpsimd.tensor_copy)
+                deal("x", k + 3, 1, nc.gpsimd.tensor_copy)
             for j in range(ROUND_TILES):
                 for s in range(SPANS):
                     project(k + 1, j, s)
@@ -362,6 +363,7 @@ def tile_tpru_pa_t_kernel(tc, h, x2f, vu, w_f, b_f, bh, bx, out):
                     scales=vu_scales[:].rearrange("d s n -> d (s n)"),
                     in_=vu_grouped[:],
                 )
+                nc.vector.tensor_scalar_mul(out=minus_bx[:], in0=bx_raw[:], scalar1=-1.0)
             invert_totals(k - 1)
             score("x", k)
             score("h2f", k)

@@ -25,6 +25,7 @@ SPANS = FEATURES // SPAN
 ROW_WORDS = FEATURES // PAIR
 
 ROUND_TILES = 2
+OPERANDS = 2
 ROUNDS = ROWS // (P * ROUND_TILES)
 ROW_BUFS = 6
 ROUND_COLS = ROUND_TILES * FEATURES
@@ -42,7 +43,7 @@ def tile_tpru_pa_t_kernel(tc, h, x2f, vu, w_f, b_f, bh, bx, out):
         dealt_pool = ctx.enter_context(tc.tile_pool(name="dealt", bufs=2))
         grouped_pool = ctx.enter_context(tc.tile_pool(name="grouped", bufs=2))
         codes_pool = ctx.enter_context(tc.tile_pool(name="codes", bufs=2))
-        tail_pool = ctx.enter_context(tc.tile_pool(name="tail", bufs=3))
+        tail_pool = ctx.enter_context(tc.tile_pool(name="tail", bufs=4))
         h2f_psum = ctx.enter_context(tc.psum_pool(name="h2f_psum", bufs=3))
         turn_psum = ctx.enter_context(tc.psum_pool(name="turn_psum", bufs=5))
         ctx.enter_context(tc.manual_schedule())
@@ -72,7 +73,7 @@ def tile_tpru_pa_t_kernel(tc, h, x2f, vu, w_f, b_f, bh, bx, out):
             rows[operand, i] = loaded
 
         def word_tiles(values, tiles):
-            return values[:].bitcast(F32).rearrange(
+            return values.bitcast(F32).rearrange(
                 "p (j g r u) -> p j g r u", j=tiles, g=SPANS, r=P, u=HALVES
             )
 
@@ -105,12 +106,17 @@ def tile_tpru_pa_t_kernel(tc, h, x2f, vu, w_f, b_f, bh, bx, out):
 
         w_rows = const.tile([P, SPANS * PACK * FEATURES], BF16)
         w_tiles = w_f.rearrange("(s c t) k -> s t c k", s=SPANS, c=P, t=PACK)
-        for s in range(SPANS):
+
+        def load_w(s):
             for t in range(PACK):
                 m = s * PACK + t
                 nc.sync.dma_start(
                     out=w_rows[:, m * FEATURES : (m + 1) * FEATURES], in_=w_tiles[s][t]
                 )
+
+        load_w(0)
+        load("h", 0)
+        load_w(1)
         bias = const.tile([P, SPANS * PACK], BF16)
         nc.gpsimd.dma_start(
             out=bias[:].rearrange("c (s t) -> c s t", t=PACK),
@@ -121,16 +127,17 @@ def tile_tpru_pa_t_kernel(tc, h, x2f, vu, w_f, b_f, bh, bx, out):
         bx_raw = const.tile([P, 1], BF16)
         nc.gpsimd.dma_start(out=bx_raw[:], in_=bx.partition_broadcast(P))
 
-        load("h", 0)
+        load("h", 1)
+        load("x", 0)
         vu_rows = const.tile([P, FEATURES], BF16)
         nc.sync.dma_start(out=vu_rows[:], in_=vu.rearrange("n s d -> n (s d)"))
-        for i in range(1, ROW_BUFS):
+        for i in range(2, ROW_BUFS):
             load("h", i)
             load("x", i - 1)
         load("x", ROW_BUFS - 1)
 
         w_grouped = const.tile([P, SPANS * PACK * FEATURES], BF16, align_bytes=64)
-        w_grouped_words = word_tiles(w_grouped, SPANS * PACK)
+        w_grouped_words = word_tiles(w_grouped[:], SPANS * PACK)
         w_codes = const.tile([P, SPANS, PACK, SPANS, P], U32, align_bytes=64)
         w_scales = const.tile([P, SPANS, PACK, SPANS, P], U8, align_bytes=64)
 
@@ -142,28 +149,27 @@ def tile_tpru_pa_t_kernel(tc, h, x2f, vu, w_f, b_f, bh, bx, out):
                 in_=w_grouped[:, m * FEATURES : (m + 2) * FEATURES],
             )
 
-        for s in range(SPANS):
-            for t in range(PACK):
+        def flip_w(s, tiles):
+            for t in tiles:
                 m = s * PACK + t
                 flip_tile(
                     loaded_words(w_rows, m),
                     w_grouped_words[:, m],
                     nc.scalar.copy if t % 2 == 0 else nc.vector.tensor_copy,
                 )
-                if t == 3:
-                    quantise_w(s, 0)
-                elif t == 1 and s > 0:
-                    quantise_w(s - 1, 2)
 
         minus_bx = const.tile([P, 1], F32)
+        score_bias = {"x": bh_raw, "h2f": bx_raw}
+
+        def new_step(i):
+            both = grouped_pool.tile([P, OPERANDS * ROUND_COLS], BF16, align_bytes=64)
+            grouped["hx", i] = both
+            grouped["h", i] = both[:, :ROUND_COLS]
+            grouped["x", i - 1] = both[:, ROUND_COLS:]
 
         def flip(operand, i, j, copy):
             if not live(i):
                 return
-            if j == 0:
-                grouped[operand, i] = grouped_pool.tile(
-                    [P, ROUND_COLS], BF16, name=operand + "_grouped", align_bytes=64
-                )
             flip_tile(
                 dealt[operand, i, j]
                 if (operand, i, j) in dealt
@@ -174,26 +180,37 @@ def tile_tpru_pa_t_kernel(tc, h, x2f, vu, w_f, b_f, bh, bx, out):
             if j == ROUND_TILES - 1:
                 load(operand, i + ROW_BUFS)
 
-        def quantise(operand, i, lo=0, hi=ROUND_TILES):
+        def quantise_hx(i):
+            first = 0 if live(i) else 1
+            end = 2 if live(i - 1) else 1
+            if first >= end:
+                return
+            shape = [P, OPERANDS, ROUND_TILES, SPANS, P]
+            words = codes_pool.tile(shape, U32, align_bytes=64)
+            plane = codes_pool.tile(shape, U8, align_bytes=64)
+            nc.vector.quantize_mx(
+                out=words[:, first:end].rearrange("k o j g r -> k (o j g r)").bitcast(FP8X4),
+                scales=plane[:, first:end].rearrange("k o j g r -> k (o j g r)"),
+                in_=grouped["hx", i][:, first * ROUND_COLS : end * ROUND_COLS],
+            )
+            codes["h", i] = words[:, 0]
+            scales["h", i] = plane[:, 0]
+            codes["x", i - 1] = words[:, 1]
+            scales["x", i - 1] = plane[:, 1]
+
+        def quantise_h2f(i, lo=0, hi=ROUND_TILES):
             if not live(i):
                 return
             if lo == 0:
-                new_codes(operand, i)
+                h2f_words = codes_pool.tile([P, ROUND_TILES, SPANS, P], U32, align_bytes=64)
+                h2f_plane = codes_pool.tile([P, ROUND_TILES, SPANS, P], U8, align_bytes=64)
+                codes["h2f", i] = h2f_words
+                scales["h2f", i] = h2f_plane
             nc.vector.quantize_mx(
-                out=codes[operand, i][:, lo:hi].rearrange("k j g r -> k (j g r)").bitcast(FP8X4),
-                scales=scales[operand, i][:, lo:hi].rearrange("k j g r -> k (j g r)"),
-                in_=grouped[operand, i][:, lo * FEATURES : hi * FEATURES],
+                out=codes["h2f", i][:, lo:hi].rearrange("k j g r -> k (j g r)").bitcast(FP8X4),
+                scales=scales["h2f", i][:, lo:hi].rearrange("k j g r -> k (j g r)"),
+                in_=grouped["h2f", i][:, lo * FEATURES : hi * FEATURES],
             )
-
-        def new_codes(operand, i):
-            words = codes_pool.tile(
-                [P, ROUND_TILES, SPANS, P], U32, name=operand + "_codes", align_bytes=64
-            )
-            plane = codes_pool.tile(
-                [P, ROUND_TILES, SPANS, P], U8, name=operand + "_scales", align_bytes=64
-            )
-            codes[operand, i] = words
-            scales[operand, i] = plane
 
         def project(i, j, s):
             if not live(i):
@@ -242,17 +259,29 @@ def tile_tpru_pa_t_kernel(tc, h, x2f, vu, w_f, b_f, bh, bx, out):
                         stop=True,
                     )
 
-        def relu(i):
+        def vector_joins(i):
+            return i % 2 == 1 or i == 0 or i >= ROUNDS - 2
+
+        def relu(operand, i):
             if not live(i):
                 return
-            ah = tail_pool.tile([P, SCORE_COLS], F32)
-            tail["ah", i] = ah
+            kept = tail_pool.tile([P, SCORE_COLS], F32, name=operand + "_relu")
+            tail[operand, i] = kept
             nc.scalar.activation(
-                out=ah[:],
-                in_=scores["x", i][:].rearrange("r j s n -> r (j s n)"),
+                out=kept[:],
+                in_=scores[operand, i][:].rearrange("r j s n -> r (j s n)"),
                 func=ACT.Relu,
-                bias=bh_raw[:, 0:1],
+                bias=score_bias[operand][:, 0:1],
                 scale=1.0,
+            )
+
+        def add(i):
+            if not live(i) or vector_joins(i):
+                return
+            both = tail_pool.tile([P, SCORE_COLS], F32)
+            tail["both", i] = both
+            nc.gpsimd.tensor_tensor(
+                out=both[:], in0=tail["x", i][:], in1=tail["h2f", i][:], op=ALU.add
             )
 
         def join(i, lo=0, hi=ROUND_TILES):
@@ -265,7 +294,7 @@ def tile_tpru_pa_t_kernel(tc, h, x2f, vu, w_f, b_f, bh, bx, out):
                 out=tail["both", i][:, lo * TILE_SCORES : hi * TILE_SCORES],
                 in0=scores["h2f", i][:, lo:hi].rearrange("r j s n -> r (j s n)"),
                 scalar=minus_bx[:, 0:1],
-                in1=tail["ah", i][:, lo * TILE_SCORES : hi * TILE_SCORES],
+                in1=tail["x", i][:, lo * TILE_SCORES : hi * TILE_SCORES],
                 op0=ALU.max,
                 op1=ALU.add,
             )
@@ -273,6 +302,7 @@ def tile_tpru_pa_t_kernel(tc, h, x2f, vu, w_f, b_f, bh, bx, out):
         def square(i, lo=0, hi=ROUND_TILES):
             if not live(i):
                 return
+            missing = bx_raw[:, 0:1] if vector_joins(i) else 0.0
             if lo == 0:
                 a2 = tail_pool.tile([P, SCORE_COLS], F32)
                 totals = tail_pool.tile([P, ROUND_TILES * SPANS], F32)
@@ -283,7 +313,7 @@ def tile_tpru_pa_t_kernel(tc, h, x2f, vu, w_f, b_f, bh, bx, out):
                     out=tail["a2", i][:, q * ROLES : (q + 1) * ROLES],
                     in_=tail["both", i][:, q * ROLES : (q + 1) * ROLES],
                     func=ACT.Square,
-                    bias=bx_raw[:, 0:1],
+                    bias=missing,
                     scale=1.0,
                     accum_out=tail["totals", i][:, q : q + 1],
                 )
@@ -333,78 +363,113 @@ def tile_tpru_pa_t_kernel(tc, h, x2f, vu, w_f, b_f, bh, bx, out):
             )
             nc.sync.dma_start(out=dram_rounds["out"][i][:, cols], in_=tail["result", i][:, cols])
 
-        flip("h", 0, 0, nc.scalar.copy)
-        flip("h", 0, 1, nc.vector.tensor_copy)
-        quantise_w(SPANS - 1, 2)
-
+        new_step(0)
+        flip_w(0, range(PACK))
+        quantise_w(0, 0)
+        for j in range(ROUND_TILES):
+            flip("h", 0, j, nc.scalar.copy)
+        quantise_w(0, 2)
+        flip_w(1, range(2))
+        quantise_hx(0)
+        flip_w(1, range(2, PACK))
+        quantise_w(1, 0)
+        quantise_w(1, 2)
+        for operand, i in (("h", 1), ("x", 0), ("h", 2)):
+            for j in range(ROUND_TILES):
+                deal(operand, i, j, nc.scalar.copy)
+        for s in range(SPANS):
+            for j in range(ROUND_TILES):
+                project(0, j, s)
+        new_step(1)
+        flip("h", 1, 0, nc.scalar.copy)
+        flip("h", 1, 1, nc.vector.tensor_copy)
+        flip("x", 0, 0, nc.scalar.copy)
+        flip("x", 0, 1, nc.vector.tensor_copy)
         vu_grouped = const.tile([P, FEATURES], BF16, align_bytes=64)
         vu_codes = const.tile([P, SPANS, ROLES], U32, align_bytes=64)
         vu_scales = const.tile([P, SPANS, ROLES], U8, align_bytes=64)
-        flip_tile(loaded_words(vu_rows, 0), word_tiles(vu_grouped, 1)[:, 0], nc.scalar.copy)
+        flip_tile(loaded_words(vu_rows, 0), word_tiles(vu_grouped[:], 1)[:, 0], nc.scalar.copy)
+        quantise_hx(1)
+        quantise_h2f(0)
+        nc.vector.quantize_mx(
+            out=vu_codes[:].rearrange("d s n -> d (s n)").bitcast(FP8X4),
+            scales=vu_scales[:].rearrange("d s n -> d (s n)"),
+            in_=vu_grouped[:],
+        )
+        nc.vector.tensor_scalar_mul(out=minus_bx[:], in0=bx_raw[:], scalar1=-1.0)
+        new_step(2)
+        for j in range(ROUND_TILES):
+            flip("h", 2, j, nc.scalar.copy)
+        for j in range(ROUND_TILES):
+            flip("x", 1, j, nc.scalar.copy)
+        for j in range(ROUND_TILES):
+            deal("h", 3, j, nc.scalar.copy)
 
-        for k in range(-2, ROUNDS - 2):
-            normalise(nc.gpsimd, k - 2)
-            square(k - 1)
-            if k >= 0:
-                deal("h", k + 4, 0, nc.scalar.copy)
-                deal("x", k + 3, 0, nc.scalar.copy)
-                deal("h", k + 4, 1, nc.gpsimd.tensor_copy)
-                deal("x", k + 3, 1, nc.gpsimd.tensor_copy)
+        for k in range(ROUNDS - 2):
+            normalise(nc.gpsimd, k - 3)
+            add(k - 1)
+            square(k - 2)
+            for j in range(ROUND_TILES):
+                if not vector_joins(k) and k >= 3:
+                    deal("x", k + 3, j, nc.gpsimd.tensor_copy)
             for j in range(ROUND_TILES):
                 for s in range(SPANS):
                     project(k + 1, j, s)
-            quantise("h", k + 2)
-            floor_totals(k - 1)
-            quantise("x", k + 1)
-            quantise("h2f", k + 1)
-            if k == -1:
-                nc.vector.quantize_mx(
-                    out=vu_codes[:].rearrange("d s n -> d (s n)").bitcast(FP8X4),
-                    scales=vu_scales[:].rearrange("d s n -> d (s n)"),
-                    in_=vu_grouped[:],
-                )
-                nc.vector.tensor_scalar_mul(out=minus_bx[:], in0=bx_raw[:], scalar1=-1.0)
-            invert_totals(k - 1)
+            floor_totals(k - 2)
+            quantise_hx(k + 2)
+            quantise_h2f(k + 1)
+            invert_totals(k - 2)
             score("x", k)
             score("h2f", k)
-            relu(k)
-            join(k)
+            relu("x", k)
+            if vector_joins(k):
+                join(k)
+            else:
+                relu("h2f", k)
+            new_step(k + 3)
             for j in range(ROUND_TILES):
                 flip("h", k + 3, j, nc.scalar.copy)
             for j in range(ROUND_TILES):
                 flip("x", k + 2, j, nc.scalar.copy)
+            for j in range(ROUND_TILES):
+                if vector_joins(k) or j == 0 or k < 1:
+                    deal("h", k + 4, j, nc.scalar.copy)
 
         last = ROUNDS - 1
-        normalise(nc.gpsimd, last - 3)
+        normalise(nc.gpsimd, last - 4)
+        square(last - 3)
         square(last - 2)
+        project(last, 0, 0)
+        project(last, 0, 1)
         score("x", last - 1)
         score("h2f", last - 1)
-        relu(last - 1)
-        quantise("x", last)
-        floor_totals(last - 2)
-        project(last, 0, 0)
-        invert_totals(last - 2)
-        normalise(nc.gpsimd, last - 2)
-        project(last, 0, 1)
-        score("x", last)
-        relu(last)
+        relu("x", last - 1)
         join(last - 1)
+        floor_totals(last - 3)
+        quantise_hx(last + 1)
+        invert_totals(last - 3)
+        normalise(nc.gpsimd, last - 3)
         project(last, 1, 0)
         square(last - 1)
-        quantise("h2f", last, 0, 1)
         project(last, 1, 1)
+        score("x", last)
+        relu("x", last)
+        quantise_h2f(last, 0, 1)
+        floor_totals(last - 2)
         score("h2f", last, 0, 1)
-        floor_totals(last - 1)
+        quantise_h2f(last, 1, 2)
+        invert_totals(last - 2)
         join(last, 0, 1)
-        quantise("h2f", last, 1, 2)
-        invert_totals(last - 1)
         score("h2f", last, 1, 2)
         square(last, 0, 1)
-        normalise(nc.vector, last - 1)
+        normalise(nc.vector, last - 2)
         join(last, 1, 2)
+        floor_totals(last - 1)
         floor_totals(last, 0, 1)
         square(last, 1, 2)
+        invert_totals(last - 1)
         invert_totals(last, 0, 1)
+        normalise(nc.vector, last - 1)
         normalise(nc.vector, last, 0, 1)
         floor_totals(last, 1, 2)
         invert_totals(last, 1, 2)

@@ -260,7 +260,7 @@ def tile_tpru_pa_t_kernel(tc, h, x2f, vu, w_f, b_f, bh, bx, out):
                     )
 
         def vector_joins(i):
-            return i % 2 == 1 or i == 0 or i >= ROUNDS - 2
+            return True
 
         def relu(operand, i):
             if not live(i):
@@ -406,38 +406,33 @@ def tile_tpru_pa_t_kernel(tc, h, x2f, vu, w_f, b_f, bh, bx, out):
             deal("h", 3, j, nc.scalar.copy)
 
         for k in range(ROUNDS - 2):
-            normalise(nc.gpsimd, k - 3)
-            add(k - 1)
-            square(k - 2)
+            normalise(nc.gpsimd, k - 2)
+            square(k - 1)
             for j in range(ROUND_TILES):
-                if not vector_joins(k) and k >= 3:
+                if k >= 2:
                     deal("x", k + 3, j, nc.gpsimd.tensor_copy)
             for j in range(ROUND_TILES):
                 for s in range(SPANS):
                     project(k + 1, j, s)
-            floor_totals(k - 2)
             quantise_hx(k + 2)
+            floor_totals(k - 1)
             quantise_h2f(k + 1)
-            invert_totals(k - 2)
+            invert_totals(k - 1)
             score("x", k)
             score("h2f", k)
             relu("x", k)
-            if vector_joins(k):
-                join(k)
-            else:
-                relu("h2f", k)
+            join(k)
             new_step(k + 3)
             for j in range(ROUND_TILES):
                 flip("h", k + 3, j, nc.scalar.copy)
             for j in range(ROUND_TILES):
                 flip("x", k + 2, j, nc.scalar.copy)
             for j in range(ROUND_TILES):
-                if vector_joins(k) or j == 0 or k < 1:
+                if j == 0:
                     deal("h", k + 4, j, nc.scalar.copy)
 
         last = ROUNDS - 1
-        normalise(nc.gpsimd, last - 4)
-        square(last - 3)
+        normalise(nc.gpsimd, last - 3)
         square(last - 2)
         project(last, 0, 0)
         project(last, 0, 1)
@@ -445,31 +440,28 @@ def tile_tpru_pa_t_kernel(tc, h, x2f, vu, w_f, b_f, bh, bx, out):
         score("h2f", last - 1)
         relu("x", last - 1)
         join(last - 1)
-        floor_totals(last - 3)
+        floor_totals(last - 2)
         quantise_hx(last + 1)
-        invert_totals(last - 3)
-        normalise(nc.gpsimd, last - 3)
+        invert_totals(last - 2)
+        normalise(nc.gpsimd, last - 2)
         project(last, 1, 0)
         square(last - 1)
         project(last, 1, 1)
         score("x", last)
         relu("x", last)
         quantise_h2f(last, 0, 1)
-        floor_totals(last - 2)
+        floor_totals(last - 1)
         score("h2f", last, 0, 1)
         quantise_h2f(last, 1, 2)
-        invert_totals(last - 2)
+        invert_totals(last - 1)
         join(last, 0, 1)
         score("h2f", last, 1, 2)
         square(last, 0, 1)
-        normalise(nc.vector, last - 2)
         join(last, 1, 2)
-        floor_totals(last - 1)
         floor_totals(last, 0, 1)
         square(last, 1, 2)
-        invert_totals(last - 1)
-        invert_totals(last, 0, 1)
         normalise(nc.vector, last - 1)
+        invert_totals(last, 0, 1)
         normalise(nc.vector, last, 0, 1)
         floor_totals(last, 1, 2)
         invert_totals(last, 1, 2)

@@ -25,7 +25,6 @@ SPANS = FEATURES // SPAN
 ROW_WORDS = FEATURES // PAIR
 
 ROUND_TILES = 2
-OPERANDS = 2
 ROUNDS = ROWS // (P * ROUND_TILES)
 ROW_BUFS = 6
 ROUND_COLS = ROUND_TILES * FEATURES
@@ -155,61 +154,44 @@ def tile_tpru_pa_t_kernel(tc, h, x2f, vu, w_f, b_f, bh, bx, out):
                 flip_tile(
                     loaded_words(w_rows, m),
                     w_grouped_words[:, m],
-                    nc.scalar.copy if t % 2 == 0 else nc.vector.tensor_copy,
+                    nc.scalar.copy,
                 )
 
         minus_bx = const.tile([P, 1], F32)
         score_bias = {"x": bh_raw, "h2f": bx_raw}
 
-        def new_step(i):
-            both = grouped_pool.tile([P, OPERANDS * ROUND_COLS], BF16, align_bytes=64)
-            grouped["hx", i] = both
-            grouped["h", i] = both[:, :ROUND_COLS]
-            grouped["x", i - 1] = both[:, ROUND_COLS:]
-
         def flip(operand, i, j, copy):
             if not live(i):
                 return
+            if j == 0:
+                grouped[operand, i] = grouped_pool.tile(
+                    [P, ROUND_COLS], BF16, name=operand + "_grouped", align_bytes=64
+                )
             flip_tile(
                 dealt[operand, i, j]
                 if (operand, i, j) in dealt
                 else loaded_words(rows[operand, i], j),
-                word_tiles(grouped[operand, i], ROUND_TILES)[:, j],
+                word_tiles(grouped[operand, i][:], ROUND_TILES)[:, j],
                 copy,
             )
             if j == ROUND_TILES - 1:
                 load(operand, i + ROW_BUFS)
 
-        def quantise_hx(i):
-            first = 0 if live(i) else 1
-            end = 2 if live(i - 1) else 1
-            if first >= end:
-                return
-            shape = [P, OPERANDS, ROUND_TILES, SPANS, P]
-            words = codes_pool.tile(shape, U32, align_bytes=64)
-            plane = codes_pool.tile(shape, U8, align_bytes=64)
-            nc.vector.quantize_mx(
-                out=words[:, first:end].rearrange("k o j g r -> k (o j g r)").bitcast(FP8X4),
-                scales=plane[:, first:end].rearrange("k o j g r -> k (o j g r)"),
-                in_=grouped["hx", i][:, first * ROUND_COLS : end * ROUND_COLS],
-            )
-            codes["h", i] = words[:, 0]
-            scales["h", i] = plane[:, 0]
-            codes["x", i - 1] = words[:, 1]
-            scales["x", i - 1] = plane[:, 1]
-
-        def quantise_h2f(i, lo=0, hi=ROUND_TILES):
+        def quantise(operand, i, lo=0, hi=ROUND_TILES):
             if not live(i):
                 return
             if lo == 0:
-                h2f_words = codes_pool.tile([P, ROUND_TILES, SPANS, P], U32, align_bytes=64)
-                h2f_plane = codes_pool.tile([P, ROUND_TILES, SPANS, P], U8, align_bytes=64)
-                codes["h2f", i] = h2f_words
-                scales["h2f", i] = h2f_plane
+                shape = [P, ROUND_TILES, SPANS, P]
+                codes[operand, i] = codes_pool.tile(
+                    shape, U32, name=operand + "_codes", align_bytes=64
+                )
+                scales[operand, i] = codes_pool.tile(
+                    shape, U8, name=operand + "_scales", align_bytes=64
+                )
             nc.vector.quantize_mx(
-                out=codes["h2f", i][:, lo:hi].rearrange("k j g r -> k (j g r)").bitcast(FP8X4),
-                scales=scales["h2f", i][:, lo:hi].rearrange("k j g r -> k (j g r)"),
-                in_=grouped["h2f", i][:, lo * FEATURES : hi * FEATURES],
+                out=codes[operand, i][:, lo:hi].rearrange("k j g r -> k (j g r)").bitcast(FP8X4),
+                scales=scales[operand, i][:, lo:hi].rearrange("k j g r -> k (j g r)"),
+                in_=grouped[operand, i][:, lo * FEATURES : hi * FEATURES],
             )
 
         def project(i, j, s):
@@ -363,14 +345,13 @@ def tile_tpru_pa_t_kernel(tc, h, x2f, vu, w_f, b_f, bh, bx, out):
             )
             nc.sync.dma_start(out=dram_rounds["out"][i][:, cols], in_=tail["result", i][:, cols])
 
-        new_step(0)
         flip_w(0, range(PACK))
         quantise_w(0, 0)
         for j in range(ROUND_TILES):
             flip("h", 0, j, nc.scalar.copy)
         quantise_w(0, 2)
         flip_w(1, range(2))
-        quantise_hx(0)
+        quantise("h", 0)
         flip_w(1, range(2, PACK))
         quantise_w(1, 0)
         quantise_w(1, 2)
@@ -380,7 +361,6 @@ def tile_tpru_pa_t_kernel(tc, h, x2f, vu, w_f, b_f, bh, bx, out):
         for s in range(SPANS):
             for j in range(ROUND_TILES):
                 project(0, j, s)
-        new_step(1)
         flip("h", 1, 0, nc.scalar.copy)
         flip("h", 1, 1, nc.vector.tensor_copy)
         flip("x", 0, 0, nc.scalar.copy)
@@ -389,15 +369,15 @@ def tile_tpru_pa_t_kernel(tc, h, x2f, vu, w_f, b_f, bh, bx, out):
         vu_codes = const.tile([P, SPANS, ROLES], U32, align_bytes=64)
         vu_scales = const.tile([P, SPANS, ROLES], U8, align_bytes=64)
         flip_tile(loaded_words(vu_rows, 0), word_tiles(vu_grouped[:], 1)[:, 0], nc.scalar.copy)
-        quantise_hx(1)
-        quantise_h2f(0)
+        quantise("h", 1)
+        quantise("x", 0)
+        quantise("h2f", 0)
         nc.vector.quantize_mx(
             out=vu_codes[:].rearrange("d s n -> d (s n)").bitcast(FP8X4),
             scales=vu_scales[:].rearrange("d s n -> d (s n)"),
             in_=vu_grouped[:],
         )
         nc.vector.tensor_scalar_mul(out=minus_bx[:], in0=bx_raw[:], scalar1=-1.0)
-        new_step(2)
         for j in range(ROUND_TILES):
             flip("h", 2, j, nc.scalar.copy)
         for j in range(ROUND_TILES):
@@ -409,26 +389,27 @@ def tile_tpru_pa_t_kernel(tc, h, x2f, vu, w_f, b_f, bh, bx, out):
             normalise(nc.gpsimd, k - 2)
             square(k - 1)
             for j in range(ROUND_TILES):
-                if k >= 2:
+                if False:
                     deal("x", k + 3, j, nc.gpsimd.tensor_copy)
-            for j in range(ROUND_TILES):
-                for s in range(SPANS):
-                    project(k + 1, j, s)
-            quantise_hx(k + 2)
+            for s in range(SPANS):
+                project(k + 1, 0, s)
+            quantise("h", k + 2)
+            for s in range(SPANS):
+                project(k + 1, 1, s)
             floor_totals(k - 1)
-            quantise_h2f(k + 1)
+            quantise("x", k + 1)
+            quantise("h2f", k + 1)
             invert_totals(k - 1)
             score("x", k)
             score("h2f", k)
             relu("x", k)
             join(k)
-            new_step(k + 3)
             for j in range(ROUND_TILES):
                 flip("h", k + 3, j, nc.scalar.copy)
             for j in range(ROUND_TILES):
                 flip("x", k + 2, j, nc.scalar.copy)
             for j in range(ROUND_TILES):
-                if j == 0:
+                if True:
                     deal("h", k + 4, j, nc.scalar.copy)
 
         last = ROUNDS - 1
@@ -441,7 +422,7 @@ def tile_tpru_pa_t_kernel(tc, h, x2f, vu, w_f, b_f, bh, bx, out):
         relu("x", last - 1)
         join(last - 1)
         floor_totals(last - 2)
-        quantise_hx(last + 1)
+        quantise("x", last)
         invert_totals(last - 2)
         normalise(nc.gpsimd, last - 2)
         project(last, 1, 0)
@@ -449,10 +430,10 @@ def tile_tpru_pa_t_kernel(tc, h, x2f, vu, w_f, b_f, bh, bx, out):
         project(last, 1, 1)
         score("x", last)
         relu("x", last)
-        quantise_h2f(last, 0, 1)
+        quantise("h2f", last, 0, 1)
         floor_totals(last - 1)
         score("h2f", last, 0, 1)
-        quantise_h2f(last, 1, 2)
+        quantise("h2f", last, 1, 2)
         invert_totals(last - 1)
         join(last, 0, 1)
         score("h2f", last, 1, 2)

@@ -420,9 +420,10 @@ def tile_tpru_pa_t_kernel(tc, h, x2f, vu, w_f, b_f, bh, bx, out):
         score("x", last - 1)
         score("h2f", last - 1)
         relu("x", last - 1)
-        join(last - 1)
-        floor_totals(last - 2)
         quantise("x", last)
+        floor_totals(last - 2)
+        quantise("h2f", last, 0, 1)
+        join(last - 1)
         invert_totals(last - 2)
         normalise(nc.gpsimd, last - 2)
         project(last, 1, 0)
@@ -430,18 +431,17 @@ def tile_tpru_pa_t_kernel(tc, h, x2f, vu, w_f, b_f, bh, bx, out):
         project(last, 1, 1)
         score("x", last)
         relu("x", last)
-        quantise("h2f", last, 0, 1)
-        floor_totals(last - 1)
         score("h2f", last, 0, 1)
+        floor_totals(last - 1)
         quantise("h2f", last, 1, 2)
         invert_totals(last - 1)
         join(last, 0, 1)
         score("h2f", last, 1, 2)
         square(last, 0, 1)
+        normalise(nc.vector, last - 1)
         join(last, 1, 2)
         floor_totals(last, 0, 1)
         square(last, 1, 2)
-        normalise(nc.vector, last - 1)
         invert_totals(last, 0, 1)
         normalise(nc.vector, last, 0, 1)
         floor_totals(last, 1, 2)

from contextlib import ExitStack

import concourse.mybir as mybir
from concourse.masks import make_identity

F32 = mybir.dt.float32
BF16 = mybir.dt.bfloat16
U32 = mybir.dt.uint32
U8 = mybir.dt.uint8
FP8X4 = mybir.dt.float8_e4m3fn_x4
ALU = mybir.AluOpType
ACT = mybir.ActivationFunctionType

P = 128
ROWS = 4096
FEATURES = 1024
ROLES = 128
EPS = 1e-12

PACK = 4
HALVES = 2
PAIR = 2
SPAN = P * PACK
SPANS = FEATURES // SPAN
ROW_WORDS = FEATURES // PAIR

ROUND_TILES = 2
ROUNDS = ROWS // (P * ROUND_TILES)
ROW_BUFS = 6
ROUND_COLS = ROUND_TILES * FEATURES
TILE_SCORES = SPANS * ROLES
SCORE_COLS = ROUND_TILES * TILE_SCORES

FLOPS = 2 * ROWS * FEATURES * FEATURES + 2 * 2 * ROWS * FEATURES * ROLES


def tile_tpru_pa_t_kernel(tc, h, x2f, vu, w_f, b_f, bh, bx, out):
    nc = tc.nc
    with ExitStack() as ctx:
        const = ctx.enter_context(tc.tile_pool(name="const", bufs=1))
        rows_pool = ctx.enter_context(tc.tile_pool(name="rows", bufs=ROW_BUFS))
        dealt_pool = ctx.enter_context(tc.tile_pool(name="dealt", bufs=2))
        grouped_pool = ctx.enter_context(tc.tile_pool(name="grouped", bufs=2))
        codes_pool = ctx.enter_context(tc.tile_pool(name="codes", bufs=2))
        tail_pool = ctx.enter_context(tc.tile_pool(name="tail", bufs=4))
        h2f_psum = ctx.enter_context(tc.psum_pool(name="h2f_psum", bufs=3))
        turn_psum = ctx.enter_context(tc.psum_pool(name="turn_psum", bufs=5))
        ctx.enter_context(tc.manual_schedule())

        dram_rounds = {
            "h": h.rearrange("(i p j) k -> i p (j k)", p=P, j=ROUND_TILES),
            "x": x2f.rearrange("(i p j) k -> i p (j k)", p=P, j=ROUND_TILES),
            "out": out.rearrange("(i p j) n s -> i p (j n s)", p=P, j=ROUND_TILES),
        }

        rows = {}
        dealt = {}
        grouped = {}
        codes = {}
        scales = {}
        scores = {}
        tail = {}

        def live(i):
            return 0 <= i < ROUNDS

        def load(operand, i):
            if not live(i):
                return
            loaded = rows_pool.tile([P, ROUND_COLS], BF16, name=operand + "_rows")
            nc.sync.dma_start(out=loaded[:], in_=dram_rounds[operand][i])
            rows[operand, i] = loaded

        def word_tiles(values, tiles):
            return values.bitcast(F32).rearrange(
                "p (j g r u) -> p j g r u", j=tiles, g=SPANS, r=P, u=HALVES
            )

        def deal(operand, i, j, copy):
            if not live(i):
                return
            sorted_words = dealt_pool.tile(
                [P, SPANS, HALVES, P], F32, name=operand + "_dealt" + str(j)
            )
            copy(
                out=sorted_words[:],
                in_=loaded_words(rows[operand, i], j),
            )
            dealt[operand, i, j] = sorted_words

        def loaded_words(values, j):
            return values[:].bitcast(F32)[:, j * ROW_WORDS : (j + 1) * ROW_WORDS].rearrange(
                "r (g p u) -> r g u p", g=SPANS, u=HALVES
            )

        def flip_tile(row_words, grouped_words, copy):
            flipped = turn_psum.tile([P, SPANS, HALVES, P], F32, tag="turn")
            for g in range(SPANS):
                for u in range(HALVES):
                    nc.tensor.transpose(flipped[:, g, u, :], row_words[:, g, u, :], identity[:])
            copy(out=grouped_words, in_=flipped[:].rearrange("p g u r -> p g r u"))

        identity = const.tile([P, P], F32)
        make_identity(nc, identity[:])

        w_rows = const.tile([P, SPANS * PACK * FEATURES], BF16)
        w_tiles = w_f.rearrange("(s c t) k -> s t c k", s=SPANS, c=P, t=PACK)

        def load_w(s):
            for t in range(PACK):
                m = s * PACK + t
                nc.sync.dma_start(
                    out=w_rows[:, m * FEATURES : (m + 1) * FEATURES], in_=w_tiles[s][t]
                )

        load_w(0)
        load("h", 0)
        load_w(1)
        bias = const.tile([P, SPANS * PACK], BF16)
        nc.gpsimd.dma_start(
            out=bias[:].rearrange("c (s t) -> c s t", t=PACK),
            in_=b_f.rearrange("(s c t) -> c s t", s=SPANS, c=P, t=PACK),
        )
        bh_raw = const.tile([P, 1], BF16)
        nc.gpsimd.dma_start(out=bh_raw[:], in_=bh.partition_broadcast(P))
        bx_raw = const.tile([P, 1], BF16)
        nc.gpsimd.dma_start(out=bx_raw[:], in_=bx.partition_broadcast(P))

        load("h", 1)
        load("x", 0)
        vu_rows = const.tile([P, FEATURES], BF16)
        nc.sync.dma_start(out=vu_rows[:], in_=vu.rearrange("n s d -> n (s d)"))
        for i in range(2, ROW_BUFS):
            load("h", i)
            load("x", i - 1)
        load("x", ROW_BUFS - 1)

        w_grouped = const.tile([P, SPANS * PACK * FEATURES], BF16, align_bytes=64)
        w_grouped_words = word_tiles(w_grouped[:], SPANS * PACK)
        w_codes = const.tile([P, SPANS, PACK, SPANS, P], U32, align_bytes=64)
        w_scales = const.tile([P, SPANS, PACK, SPANS, P], U8, align_bytes=64)

        def quantise_w(s, t):
            m = s * PACK + t
            nc.vector.quantize_mx(
                out=w_codes[:, s, t : t + 2].rearrange("k t g c -> k (t g c)").bitcast(FP8X4),
                scales=w_scales[:, s, t : t + 2].rearrange("k t g c -> k (t g c)"),
                in_=w_grouped[:, m * FEATURES : (m + 2) * FEATURES],
            )

        def flip_w(s, tiles):
            for t in tiles:
                m = s * PACK + t
                flip_tile(
                    loaded_words(w_rows, m),
                    w_grouped_words[:, m],
                    nc.scalar.copy,
                )

        minus_bx = const.tile([P, 1], F32)
        score_bias = {"x": bh_raw, "h2f": bx_raw}

        def flip(operand, i, j, copy):
            if not live(i):
                return
            if j == 0:
                grouped[operand, i] = grouped_pool.tile(
                    [P, ROUND_COLS], BF16, name=operand + "_grouped", align_bytes=64
                )
            flip_tile(
                dealt[operand, i, j]
                if (operand, i, j) in dealt
                else loaded_words(rows[operand, i], j),
                word_tiles(grouped[operand, i][:], ROUND_TILES)[:, j],
                copy,
            )
            if j == ROUND_TILES - 1:
                load(operand, i + ROW_BUFS)

        def quantise(operand, i, lo=0, hi=ROUND_TILES):
            if not live(i):
                return
            if lo == 0:
                shape = [P, ROUND_TILES, SPANS, P]
                codes[operand, i] = codes_pool.tile(
                    shape, U32, name=operand + "_codes", align_bytes=64
                )
                scales[operand, i] = codes_pool.tile(
                    shape, U8, name=operand + "_scales", align_bytes=64
                )
            nc.vector.quantize_mx(
                out=codes[operand, i][:, lo:hi].rearrange("k j g r -> k (j g r)").bitcast(FP8X4),
                scales=scales[operand, i][:, lo:hi].rearrange("k j g r -> k (j g r)"),
                in_=grouped[operand, i][:, lo * FEATURES : hi * FEATURES],
            )

        def project(i, j, s):
            if not live(i):
                return
            if (j, s) == (0, 0):
                h2f_grouped = grouped_pool.tile([P, ROUND_COLS], BF16, align_bytes=64)
                grouped["h2f", i] = h2f_grouped
            sums = h2f_psum.tile([P, PACK, P], F32)
            for t in range(PACK):
                for g in range(SPANS):
                    nc.tensor.matmul_mx(
                        out=sums[:, t, :],
                        lhsT=w_codes[:, s, t, g, :].bitcast(FP8X4),
                        lhsT_scale=w_scales[:, s, t, g, :],
                        rhs=codes["h", i][:, j, g, :].bitcast(FP8X4),
                        rhs_scale=scales["h", i][:, j, g, :],
                        start=(g == 0),
                        stop=(g == SPANS - 1),
                    )
            nc.vector.tensor_tensor(
                out=grouped["h2f", i][:].rearrange(
                    "c (j s r t) -> c j s r t", j=ROUND_TILES, s=SPANS, r=P, t=PACK
                )[:, j, s],
                in0=sums[:].rearrange("c t r -> c r t"),
                in1=bias[:, s * PACK : (s + 1) * PACK].unsqueeze(1).to_broadcast([P, P, PACK]),
                op=ALU.add,
            )

        def score(operand, i, lo=0, hi=ROUND_TILES):
            if not live(i):
                return
            if lo == 0:
                bank = turn_psum.tile(
                    [P, ROUND_TILES, SPANS, ROLES], F32, name=operand + "_scores", tag="turn"
                )
                scores[operand, i] = bank
            for j in range(lo, hi):
                for s in range(SPANS):
                    nc.tensor.matmul_mx(
                        out=scores[operand, i][:, j, s, :],
                        lhsT=codes[operand, i][:, j, s, :].bitcast(FP8X4),
                        lhsT_scale=scales[operand, i][:, j, s, :],
                        rhs=vu_codes[:, s, :].bitcast(FP8X4),
                        rhs_scale=vu_scales[:, s, :],
                        start=True,
                        stop=True,
                    )

        def vector_joins(i):
            return True

        def relu(operand, i):
            if not live(i):
                return
            kept = tail_pool.tile([P, SCORE_COLS], F32, name=operand + "_relu")
            tail[operand, i] = kept
            nc.scalar.activation(
                out=kept[:],
                in_=scores[operand, i][:].rearrange("r j s n -> r (j s n)"),
                func=ACT.Relu,
                bias=score_bias[operand][:, 0:1],
                scale=1.0,
            )

        def add(i):
            if not live(i) or vector_joins(i):
                return
            both = tail_pool.tile([P, SCORE_COLS], F32)
            tail["both", i] = both
            nc.gpsimd.tensor_tensor(
                out=both[:], in0=tail["x", i][:], in1=tail["h2f", i][:], op=ALU.add
            )

        def join(i, lo=0, hi=ROUND_TILES):
            if not live(i):
                return
            if lo == 0:
                both = tail_pool.tile([P, SCORE_COLS], F32)
                tail["both", i] = both
            nc.vector.scalar_tensor_tensor(
                out=tail["both", i][:, lo * TILE_SCORES : hi * TILE_SCORES],
                in0=scores["h2f", i][:, lo:hi].rearrange("r j s n -> r (j s n)"),
                scalar=minus_bx[:, 0:1],
                in1=tail["x", i][:, lo * TILE_SCORES : hi * TILE_SCORES],
                op0=ALU.max,
                op1=ALU.add,
            )

        def square(i, lo=0, hi=ROUND_TILES):
            if not live(i):
                return
            missing = bx_raw[:, 0:1] if vector_joins(i) else 0.0
            if lo == 0:
                a2 = tail_pool.tile([P, SCORE_COLS], F32)
                totals = tail_pool.tile([P, ROUND_TILES * SPANS], F32)
                tail["a2", i] = a2
                tail["totals", i] = totals
            for q in range(lo * SPANS, hi * SPANS):
                nc.scalar.activation(
                    out=tail["a2", i][:, q * ROLES : (q + 1) * ROLES],
                    in_=tail["both", i][:, q * ROLES : (q + 1) * ROLES],
                    func=ACT.Square,
                    bias=missing,
                    scale=1.0,
                    accum_out=tail["totals", i][:, q : q + 1],
                )

        def floor_totals(i, lo=0, hi=ROUND_TILES):
            if not live(i):
                return
            if lo == 0:
                floored = tail_pool.tile([P, ROUND_TILES * SPANS], F32)
                tail["floored", i] = floored
            nc.vector.tensor_scalar_max(
                out=tail["floored", i][:, lo * SPANS : hi * SPANS],
                in0=tail["totals", i][:, lo * SPANS : hi * SPANS],
                scalar1=EPS,
            )

        def invert_totals(i, lo=0, hi=ROUND_TILES):
            if not live(i):
                return
            if lo == 0:
                inverse = tail_pool.tile([P, ROUND_TILES * SPANS], F32)
                tail["inverse", i] = inverse
            nc.vector.reciprocal(
                out=tail["inverse", i][:, lo * SPANS : hi * SPANS],
                in_=tail["floored", i][:, lo * SPANS : hi * SPANS],
            )

        def normalise(helper, i, lo=0, hi=ROUND_TILES):
            if not live(i):
                return
            if lo == 0:
                result = tail_pool.tile([P, SCORE_COLS], F32)
                tail["result", i] = result
            cols = slice(lo * TILE_SCORES, hi * TILE_SCORES)
            helper.tensor_tensor(
                out=tail["result", i][:, cols].rearrange(
                    "r (j n s) -> r j n s", j=hi - lo, n=ROLES, s=SPANS
                ),
                in0=tail["a2", i][:, cols].rearrange(
                    "r (j s n) -> r j n s", j=hi - lo, s=SPANS, n=ROLES
                ),
                in1=tail["inverse", i][:, lo * SPANS : hi * SPANS]
                .rearrange("r (j s) -> r j s", s=SPANS)
                .unsqueeze(2)
                .to_broadcast([P, hi - lo, ROLES, SPANS]),
                op=ALU.mult,
            )
            nc.sync.dma_start(out=dram_rounds["out"][i][:, cols], in_=tail["result", i][:, cols])

        flip_w(0, range(PACK))
        quantise_w(0, 0)
        for j in range(ROUND_TILES):
            flip("h", 0, j, nc.scalar.copy)
        quantise_w(0, 2)
        flip_w(1, range(2))
        quantise("h", 0)
        flip_w(1, range(2, PACK))
        quantise_w(1, 0)
        quantise_w(1, 2)
        for operand, i in (("h", 1), ("x", 0), ("h", 2)):
            for j in range(ROUND_TILES):
                deal(operand, i, j, nc.scalar.copy)
        for s in range(SPANS):
            for j in range(ROUND_TILES):
                project(0, j, s)
        flip("h", 1, 0, nc.scalar.copy)
        flip("h", 1, 1, nc.vector.tensor_copy)
        flip("x", 0, 0, nc.scalar.copy)
        flip("x", 0, 1, nc.vector.tensor_copy)
        vu_grouped = const.tile([P, FEATURES], BF16, align_bytes=64)
        vu_codes = const.tile([P, SPANS, ROLES], U32, align_bytes=64)
        vu_scales = const.tile([P, SPANS, ROLES], U8, align_bytes=64)
        flip_tile(loaded_words(vu_rows, 0), word_tiles(vu_grouped[:], 1)[:, 0], nc.scalar.copy)
        quantise("h", 1)
        quantise("x", 0)
        quantise("h2f", 0)
        nc.vector.quantize_mx(
            out=vu_codes[:].rearrange("d s n -> d (s n)").bitcast(FP8X4),
            scales=vu_scales[:].rearrange("d s n -> d (s n)"),
            in_=vu_grouped[:],
        )
        nc.vector.tensor_scalar_mul(out=minus_bx[:], in0=bx_raw[:], scalar1=-1.0)
        for j in range(ROUND_TILES):
            flip("h", 2, j, nc.scalar.copy)
        for j in range(ROUND_TILES):
            flip("x", 1, j, nc.scalar.copy)
        for j in range(ROUND_TILES):
            deal("h", 3, j, nc.scalar.copy)

        for k in range(ROUNDS - 2):
            normalise(nc.gpsimd, k - 2)
            square(k - 1)
            for j in range(ROUND_TILES):
                if False:
                    deal("x", k + 3, j, nc.gpsimd.tensor_copy)
            for s in range(SPANS):
                project(k + 1, 0, s)
            quantise("h", k + 2)
            for s in range(SPANS):
                project(k + 1, 1, s)
            floor_totals(k - 1)
            quantise("x", k + 1)
            quantise("h2f", k + 1)
            invert_totals(k - 1)
            score("x", k)
            score("h2f", k)
            relu("x", k)
            join(k)
            for j in range(ROUND_TILES):
                flip("h", k + 3, j, nc.scalar.copy)
            for j in range(ROUND_TILES):
                flip("x", k + 2, j, nc.scalar.copy)
            for j in range(ROUND_TILES):
                if True:
                    deal("h", k + 4, j, nc.scalar.copy)

        last = ROUNDS - 1
        normalise(nc.gpsimd, last - 3)
        square(last - 2)
        project(last, 0, 0)
        project(last, 0, 1)
        score("x", last - 1)
        score("h2f", last - 1)
        relu("x", last - 1)
        quantise("x", last)
        floor_totals(last - 2)
        quantise("h2f", last, 0, 1)
        join(last - 1)
        invert_totals(last - 2)
        normalise(nc.gpsimd, last - 2)
        project(last, 1, 0)
        square(last - 1)
        project(last, 1, 1)
        score("x", last)
        relu("x", last)
        score("h2f", last, 0, 1)
        floor_totals(last - 1)
        quantise("h2f", last, 1, 2)
        invert_totals(last - 1)
        join(last, 0, 1)
        score("h2f", last, 1, 2)
        square(last, 0, 1)
        normalise(nc.vector, last - 1)
        join(last, 1, 2)
        floor_totals(last, 0, 1)
        square(last, 1, 2)
        invert_totals(last, 0, 1)
        normalise(nc.vector, last, 0, 1)
        floor_totals(last, 1, 2)
        invert_totals(last, 1, 2)
        normalise(nc.vector, last, 1, 2)
